import numpy as np
import ml_dtypes


def mxq(x, axis, fmt="e4m3"):
    dtype, down = {"e4m3": (ml_dtypes.float8_e4m3fn, 7), "e5m2": (ml_dtypes.float8_e5m2, 14)}[fmt]
    v = np.moveaxis(np.asarray(x, np.float32).astype(ml_dtypes.bfloat16).astype(np.float64), axis, -1)
    blocks = v.reshape(v.shape[:-1] + (-1, 32))
    amax = np.abs(blocks).max(-1, keepdims=True)
    byte = np.maximum(np.where(amax > 0, np.frexp(amax)[1] - 1 + 127, 0) - down, 1)
    scale = np.exp2(byte - 127.0)
    codes = (blocks / scale).astype(np.float32).astype(dtype).astype(np.float64)
    return np.moveaxis((codes * scale).reshape(v.shape), -1, axis)


WIDE = False


def mx_kscale(k):
    if not WIDE:
        return np.ones(k)
    levels = np.array([10, -10, 5, -5, 0])
    if k % 512:
        return np.exp2(np.random.permutation(np.resize(levels, k // 32))).repeat(32)
    a = np.empty((k // 512, 16))
    for p in range(k // 512):
        a[p, :8] = np.random.permutation(np.resize(levels, 8))
        for g in range(8):
            far = levels[np.abs(levels - a[p, g]) >= 10]
            a[p, g + 8] = far[np.random.randint(len(far))]
    return np.exp2(a.ravel()).repeat(32)


BF16 = ml_dtypes.bfloat16


def bf(x):
    return np.asarray(x, np.float32).astype(BF16)


def f64(x):
    return np.asarray(x).astype(np.float64)


B, C_IN, C_OUT, H, W = 2, 8192, 64, 16, 32
P = 4
G = P * P


def setup_inputs():
    s = mx_kscale(C_IN)
    bound = np.sqrt(6.0 / (C_IN + C_OUT))
    return {"x": bf(np.random.standard_normal((B, C_IN, H, W)) * s[None, :, None, None]),
            "Wg": bf(np.random.uniform(-bound, bound, (G, C_OUT, C_IN)) / s[None, None, :]),
            "bg": bf(np.random.standard_normal((G, C_OUT)) * 0.25)}


def reference(x, Wg, bg):
    Bb, C, Hh, Ww = x.shape
    H4, W4 = Hh // P, Ww // P
    xq = mxq(f64(x), 1, "e4m3")
    wq = mxq(f64(Wg), 2, "e4m3")
    xg = xq.reshape(Bb, C, H4, P, W4, P).transpose(0, 2, 4, 3, 5, 1)
    xg = xg.reshape(Bb * H4 * W4, G, C).transpose(1, 0, 2)
    y = xg @ wq.transpose(0, 2, 1)
    O = y.shape[-1]
    y = y.transpose(1, 0, 2).reshape(Bb, H4, W4, G, O) + f64(bg)
    y = y.reshape(Bb, H4, W4, P, P, O).transpose(0, 5, 1, 3, 2, 4)
    return y.reshape(Bb, O, Hh, Ww)

@@ -1,0 +1,190 @@
+import concourse.mybir as mybir
+from concourse.masks import make_identity
+
+FLOPS = 2 * 16 * 64 * 64 * 8192
+
+F32 = mybir.dt.float32
+BF16 = mybir.dt.bfloat16
+U32 = mybir.dt.uint32
+U8 = mybir.dt.uint8
+FP8X4 = mybir.dt.float8_e4m3fn_x4
+
+P = 128
+PACK = 4
+K_PASS = P * PACK
+
+BATCH, CHANNELS, OUT_CH, ROWS, COLS = 2, 8192, 64, 16, 32
+PIXELS = ROWS * COLS
+PASSES = CHANNELS // K_PASS
+PIECE = 4
+OPERANDS = 8
+
+
+def tile_groupwiselinearprojector_k_kernel(tc, x, Wg, bg, out):
+    nc = tc.nc
+    w_rows = Wg.rearrange("g o k -> (g o) k").rearrange("(l z e p) k -> l e p z k", l=2, z=2, e=2)
+
+    with (
+        tc.tile_pool(name="consts", bufs=1) as consts,
+        tc.tile_pool(name="raw", bufs=6) as raw,
+        tc.tile_pool(name="grouped", bufs=4) as grouped,
+        tc.tile_pool(name="w_ops", bufs=5) as w_ops,
+        tc.psum_pool(name="psum_t", bufs=4) as psum_t,
+        tc.psum_pool(name="psum_acc", bufs=4) as psum_acc,
+    ):
+        ident = consts.tile([P, P], F32)
+        make_identity(nc, ident[:])
+
+        bg_sb = consts.tile([OPERANDS, P], BF16)
+        for l in range(2):
+            nc.scalar.dma_start(
+                out=bg_sb[4 * l : 4 * l + 4, :].rearrange("i (z o) -> i z o", z=2),
+                in_=bg.rearrange("(l z i) o -> l i z o", l=2, z=2)[l],
+            )
+        bias_rows = consts.tile([P, P], F32)
+        nc.vector.memset(bias_rows[:], 0.0)
+        nc.vector.tensor_copy(out=bias_rows[0:OPERANDS, :], in_=bg_sb[:])
+        bias_ps = psum_t.tile([P, 4 * P], F32, tag="wt")
+        nc.tensor.transpose(bias_ps[:, 0:P], bias_rows[:], ident[:])
+        bias_sb = consts.tile([P, OPERANDS], F32)
+        nc.vector.tensor_copy(out=bias_sb[:], in_=bias_ps[:, 0:OPERANDS])
+
+        x_codes = consts.tile([P, PASSES, OPERANDS * P], U32, align_bytes=64)
+        x_scales = consts.tile([P, PASSES, OPERANDS * P], U8, align_bytes=64)
+        result = consts.tile([P, 2, 4, 8, 2, 8], F32)
+        out_sb = consts.tile([P, BATCH * PIXELS // 2], F32)
+
+        raw_x, grouped_x = {}, {}
+        raw_w, grouped_w = {}, {}
+        w_operand = {}
+        acc = {}
+
+        pieces = [(a, first, PIECE) for a in range(4) for first in range(0, PASSES, PIECE)]
+        pieces = pieces[:-1] + [(3, first, 1) for first in range(PASSES - PIECE, PASSES)]
+
+        def load_x(c):
+            raw_x[c] = raw.tile([P, BATCH, PACK, PIXELS], BF16, name="raw_x", tag="raw")
+            for b in range(BATCH):
+                nc.sync.dma_start(
+                    out=raw_x[c][:, b].rearrange("p t x -> p (t x)"),
+                    in_=x[b, c * K_PASS : (c + 1) * K_PASS].rearrange("(p t) r w -> p (t r w)", t=PACK),
+                )
+
+        def regroup_x(c):
+            grouped_x[c] = grouped.tile([P, 2, 4, P, PACK], BF16, align_bytes=64, name="grouped_x", tag="grouped")
+            src = raw_x[c][:].rearrange("p b t (h l m i) -> p b l h m t i", h=4, l=2, i=4)
+            dst = grouped_x[c][:].rearrange("p l i (b h m) t -> p b l h m t i", b=BATCH, h=4)
+            for l in range(2):
+                nc.vector.tensor_copy(out=dst[:, 0, l], in_=src[:, 0, l])
+                for h in range(4):
+                    nc.scalar.copy(out=dst[:, 1, l, h], in_=src[:, 1, l, h])
+
+        def quantise_x(c):
+            nc.vector.quantize_mx(
+                out=x_codes[:, c, :].bitcast(FP8X4),
+                scales=x_scales[:, c, :],
+                in_=grouped_x[c][:].rearrange("p l i m t -> p (l i m t)"),
+            )
+
+        def load_w(q):
+            a, first, passes = pieces[q]
+            raw_w[q] = raw.tile([P, 2 * passes * K_PASS], BF16, name="raw_w", tag="raw")
+            nc.sync.dma_start(
+                out=raw_w[q][:].rearrange("p (z k) -> p z k", z=2),
+                in_=w_rows[a // 2, a % 2][:, :, first * K_PASS : (first + passes) * K_PASS],
+            )
+
+        def transpose_w(q):
+            a, first, passes = pieces[q]
+            raw_words = raw_w[q][:].bitcast(F32).rearrange("p (z c q u) -> p z c q u", z=2, c=passes, u=2)
+            grouped_w[q] = grouped.tile([P, passes * 2 * P * PACK], BF16, align_bytes=64, name="grouped_w", tag="grouped")
+            grouped_words = grouped_w[q][:].bitcast(F32).rearrange(
+                "p (c g z o u) -> p c g z o u", c=passes, g=2, z=2, o=OUT_CH
+            )
+            for c in range(passes):
+                wt = psum_t.tile([P, 2, 2, P], F32, tag="wt")
+                for z in range(2):
+                    for u in range(2):
+                        nc.tensor.transpose(wt[:, z, u, :], raw_words[:, z, c, :, u], ident[:])
+                copy = nc.vector.tensor_copy if (first + c) % 4 == 3 else nc.scalar.copy
+                for z in range(2):
+                    copy(
+                        out=grouped_words[:, c, :, z, :, :],
+                        in_=wt[:, z].rearrange("p u (g o) -> p g o u", g=2),
+                    )
+
+        def quantise_w(q):
+            a, first, passes = pieces[q]
+            w_codes = w_ops.tile([P, passes * 2 * P], U32, align_bytes=64)
+            w_scales = w_ops.tile([P, passes * 2 * P], U8, align_bytes=64)
+            nc.vector.quantize_mx(out=w_codes[:].bitcast(FP8X4), scales=w_scales[:], in_=grouped_w[q][:])
+            for c in range(passes):
+                cols = slice(c * 2 * P, (c + 1) * 2 * P)
+                w_operand[(a, first + c)] = (w_codes[:, cols], w_scales[:, cols])
+
+        def multiply(q):
+            a, first, passes = pieces[q]
+            for g in range(2):
+                if first == 0:
+                    acc[(a, g)] = psum_acc.tile([P, P], F32, name="acc")
+                pair = 4 * (a // 2) + 2 * (a % 2) + g
+                for c in range(first, first + passes):
+                    w_codes, w_scales = w_operand[(a, c)]
+                    m_cols = slice(g * P, (g + 1) * P)
+                    n_cols = slice(pair * P, (pair + 1) * P)
+                    nc.tensor.matmul_mx(
+                        out=acc[(a, g)][:],
+                        lhsT=w_codes[:, m_cols].bitcast(FP8X4),
+                        lhsT_scale=w_scales[:, m_cols],
+                        rhs=x_codes[:, c, n_cols].bitcast(FP8X4),
+                        rhs_scale=x_scales[:, c, n_cols],
+                        start=(c == 0),
+                        stop=(c == PASSES - 1),
+                    )
+
+        def add_bias(q):
+            if not 0 <= q < len(pieces):
+                return
+            a, first, passes = pieces[q]
+            if first + passes < PASSES:
+                return
+            for g in range(2):
+                l, i = a // 2, 2 * (a % 2) + g
+                nc.vector.tensor_scalar_add(
+                    out=result[:, l, i].rearrange("p n z w -> p (n z w)"),
+                    in0=acc[(a, g)][:],
+                    scalar1=bias_sb[:, 4 * l + i : 4 * l + i + 1],
+                )
+
+        with tc.manual_schedule():
+            for c in range(PASSES + 1):
+                if c < PASSES:
+                    load_x(c)
+                    regroup_x(c)
+                if c >= 1:
+                    quantise_x(c - 1)
+            for q in range(len(pieces) + 2):
+                if q < len(pieces):
+                    load_w(q)
+                if 0 <= q - 1 < len(pieces):
+                    quantise_w(q - 1)
+                if q < len(pieces):
+                    transpose_w(q)
+                if 0 <= q - 1 < len(pieces):
+                    multiply(q - 1)
+                add_bias(q - 2)
+
+        for z in range(2):
+            rows = slice(z * OUT_CH, (z + 1) * OUT_CH)
+            copy = nc.vector.tensor_copy if z == 0 else nc.scalar.copy
+            for l in range(2):
+                copy(
+                    out=out_sb[rows, :].rearrange("p (n l w i) -> p l n w i", l=2, w=8, i=4)[:, l],
+                    in_=result[rows, l, :, :, z, :].rearrange("p i n w -> p n w i"),
+                )
+            for b in range(BATCH):
+                queue = nc.sync if b == 0 else nc.scalar
+                queue.dma_start(
+                    out=out[b].rearrange("o (m z) c -> z o m c", z=2)[z],
+                    in_=out_sb[rows, b * 256 : (b + 1) * 256].rearrange("p (m c) -> p m c", c=COLS),
+                )

@@ -8,6 +8,7 @@ BF16 = mybir.dt.bfloat16
 U32 = mybir.dt.uint32
 U8 = mybir.dt.uint8
 FP8X4 = mybir.dt.float8_e4m3fn_x4
+IDENTITY = mybir.ActivationFunctionType.Identity
 
 P = 128
 PACK = 4
@@ -17,7 +18,9 @@ BATCH, CHANNELS, OUT_CH, ROWS, COLS = 2, 8192, 64, 16, 32
 PIXELS = ROWS * COLS
 PASSES = CHANNELS // K_PASS
 PIECE = 4
-OPERANDS = 8
+PIECES = 4 * (PASSES // PIECE)
+PAIRS = 8
+EARLY = 10
 
 
 def tile_groupwiselinearprojector_k_kernel(tc, x, Wg, bg, out):
@@ -28,39 +31,38 @@ def tile_groupwiselinearprojector_k_kernel(tc, x, Wg, bg, out):
         tc.tile_pool(name="consts", bufs=1) as consts,
         tc.tile_pool(name="raw", bufs=6) as raw,
         tc.tile_pool(name="grouped", bufs=4) as grouped,
-        tc.tile_pool(name="w_ops", bufs=5) as w_ops,
-        tc.psum_pool(name="psum_t", bufs=4) as psum_t,
-        tc.psum_pool(name="psum_acc", bufs=4) as psum_acc,
+        tc.tile_pool(name="w_ops", bufs=PIECES) as w_ops,
+        tc.tile_pool(name="x_ops", bufs=EARLY + 3) as x_ops,
+        tc.psum_pool(name="psum", bufs=8) as psum,
     ):
         ident = consts.tile([P, P], F32)
         make_identity(nc, ident[:])
 
-        bg_sb = consts.tile([OPERANDS, P], BF16)
+        bg_sb = consts.tile([PAIRS, P], BF16)
         for l in range(2):
             nc.scalar.dma_start(
                 out=bg_sb[4 * l : 4 * l + 4, :].rearrange("i (z o) -> i z o", z=2),
                 in_=bg.rearrange("(l z i) o -> l i z o", l=2, z=2)[l],
             )
         bias_rows = consts.tile([P, P], F32)
-        nc.vector.memset(bias_rows[:], 0.0)
-        nc.vector.tensor_copy(out=bias_rows[0:OPERANDS, :], in_=bg_sb[:])
-        bias_ps = psum_t.tile([P, 4 * P], F32, tag="wt")
-        nc.tensor.transpose(bias_ps[:, 0:P], bias_rows[:], ident[:])
-        bias_sb = consts.tile([P, OPERANDS], F32)
-        nc.vector.tensor_copy(out=bias_sb[:], in_=bias_ps[:, 0:OPERANDS])
+        bias_sb = consts.tile([P, PAIRS], F32)
 
-        x_codes = consts.tile([P, PASSES, OPERANDS * P], U32, align_bytes=64)
-        x_scales = consts.tile([P, PASSES, OPERANDS * P], U8, align_bytes=64)
-        result = consts.tile([P, 2, 4, 8, 2, 8], F32)
-        out_sb = consts.tile([P, BATCH * PIXELS // 2], F32)
+        result = [consts.tile([P, 4, 8, 2, 8], F32, name=f"result_{l}") for l in range(2)]
+        out_sb = [consts.tile([P, 8, COLS], F32, name=f"out_sb_{l}") for l in range(2)]
 
-        raw_x, grouped_x = {}, {}
+        raw_x, grouped_x, x_operand = {}, {}, {}
         raw_w, grouped_w = {}, {}
         w_operand = {}
         acc = {}
 
-        pieces = [(a, first, PIECE) for a in range(4) for first in range(0, PASSES, PIECE)]
-        pieces = pieces[:-1] + [(3, first, 1) for first in range(PASSES - PIECE, PASSES)]
+        units = []
+        early = 0
+        for q in range(PIECES):
+            while early * PIECES <= q * EARLY and early < EARLY:
+                units.append(("x", early))
+                early += 1
+            units.append(("w", q))
+        units += [("x", c) for c in range(early, PASSES)]
 
         def load_x(c):
             raw_x[c] = raw.tile([P, BATCH, PACK, PIXELS], BF16, name="raw_x", tag="raw")
@@ -70,121 +72,146 @@ def tile_groupwiselinearprojector_k_kernel(tc, x, Wg, bg, out):
                     in_=x[b, c * K_PASS : (c + 1) * K_PASS].rearrange("(p t) r w -> p (t r w)", t=PACK),
                 )
 
-        def regroup_x(c):
+        def regroup_x(c, on_scalar):
             grouped_x[c] = grouped.tile([P, 2, 4, P, PACK], BF16, align_bytes=64, name="grouped_x", tag="grouped")
             src = raw_x[c][:].rearrange("p b t (h l m i) -> p b l h m t i", h=4, l=2, i=4)
             dst = grouped_x[c][:].rearrange("p l i (b h m) t -> p b l h m t i", b=BATCH, h=4)
-            for l in range(2):
-                nc.vector.tensor_copy(out=dst[:, 0, l], in_=src[:, 0, l])
-                for h in range(4):
-                    nc.scalar.copy(out=dst[:, 1, l, h], in_=src[:, 1, l, h])
+            for b in range(BATCH):
+                for l in range(2):
+                    if (b, l) in on_scalar:
+                        for h in range(4):
+                            nc.scalar.copy(out=dst[:, b, l, h], in_=src[:, b, l, h])
+                    else:
+                        nc.vector.tensor_copy(out=dst[:, b, l], in_=src[:, b, l])
 
-        def quantise_x(c):
-            nc.vector.quantize_mx(
-                out=x_codes[:, c, :].bitcast(FP8X4),
-                scales=x_scales[:, c, :],
-                in_=grouped_x[c][:].rearrange("p l i m t -> p (l i m t)"),
-            )
+        def quantise_x(c, halves):
+            x_codes = x_ops.tile([P, PAIRS * P], U32, align_bytes=64)
+            x_scales = x_ops.tile([P, PAIRS * P], U8, align_bytes=64)
+            x_operand[c] = (x_codes, x_scales)
+            flat = grouped_x[c][:].rearrange("p l i m t -> p (l i m t)")
+            cols = PAIRS * P // halves
+            for half in range(halves):
+                nc.vector.quantize_mx(
+                    out=x_codes[:, half * cols : (half + 1) * cols].bitcast(FP8X4),
+                    scales=x_scales[:, half * cols : (half + 1) * cols],
+                    in_=flat[:, half * cols * PACK : (half + 1) * cols * PACK],
+                )
 
         def load_w(q):
-            a, first, passes = pieces[q]
-            raw_w[q] = raw.tile([P, 2 * passes * K_PASS], BF16, name="raw_w", tag="raw")
+            a, first = q // 4, PIECE * (q % 4)
+            raw_w[q] = raw.tile([P, 2 * PIECE * K_PASS], BF16, name="raw_w", tag="raw")
             nc.sync.dma_start(
                 out=raw_w[q][:].rearrange("p (z k) -> p z k", z=2),
-                in_=w_rows[a // 2, a % 2][:, :, first * K_PASS : (first + passes) * K_PASS],
+                in_=w_rows[a // 2, a % 2][:, :, first * K_PASS : (first + PIECE) * K_PASS],
             )
 
         def transpose_w(q):
-            a, first, passes = pieces[q]
-            raw_words = raw_w[q][:].bitcast(F32).rearrange("p (z c q u) -> p z c q u", z=2, c=passes, u=2)
-            grouped_w[q] = grouped.tile([P, passes * 2 * P * PACK], BF16, align_bytes=64, name="grouped_w", tag="grouped")
+            raw_words = raw_w[q][:].bitcast(F32).rearrange("p (z c q u) -> p z c q u", z=2, c=PIECE, u=2)
+            grouped_w[q] = grouped.tile([P, PIECE * 2 * P * PACK], BF16, align_bytes=64, name="grouped_w", tag="grouped")
             grouped_words = grouped_w[q][:].bitcast(F32).rearrange(
-                "p (c g z o u) -> p c g z o u", c=passes, g=2, z=2, o=OUT_CH
+                "p (c g z o u) -> p c g z o u", c=PIECE, g=2, z=2, o=OUT_CH
             )
-            for c in range(passes):
-                wt = psum_t.tile([P, 2, 2, P], F32, tag="wt")
+            for c in range(PIECE):
+                wt = psum.tile([P, 2, 2, P], F32, name="wt", tag="bank")
                 for z in range(2):
                     for u in range(2):
                         nc.tensor.transpose(wt[:, z, u, :], raw_words[:, z, c, :, u], ident[:])
-                copy = nc.vector.tensor_copy if (first + c) % 4 == 3 else nc.scalar.copy
                 for z in range(2):
-                    copy(
+                    nc.scalar.copy(
                         out=grouped_words[:, c, :, z, :, :],
                         in_=wt[:, z].rearrange("p u (g o) -> p g o u", g=2),
                     )
 
         def quantise_w(q):
-            a, first, passes = pieces[q]
-            w_codes = w_ops.tile([P, passes * 2 * P], U32, align_bytes=64)
-            w_scales = w_ops.tile([P, passes * 2 * P], U8, align_bytes=64)
+            a, first = q // 4, PIECE * (q % 4)
+            w_codes = w_ops.tile([P, PIECE * 2 * P], U32, align_bytes=64)
+            w_scales = w_ops.tile([P, PIECE * 2 * P], U8, align_bytes=64)
             nc.vector.quantize_mx(out=w_codes[:].bitcast(FP8X4), scales=w_scales[:], in_=grouped_w[q][:])
-            for c in range(passes):
+            for c in range(PIECE):
                 cols = slice(c * 2 * P, (c + 1) * 2 * P)
                 w_operand[(a, first + c)] = (w_codes[:, cols], w_scales[:, cols])
 
-        def multiply(q):
-            a, first, passes = pieces[q]
-            for g in range(2):
-                if first == 0:
-                    acc[(a, g)] = psum_acc.tile([P, P], F32, name="acc")
-                pair = 4 * (a // 2) + 2 * (a % 2) + g
-                for c in range(first, first + passes):
-                    w_codes, w_scales = w_operand[(a, c)]
-                    m_cols = slice(g * P, (g + 1) * P)
-                    n_cols = slice(pair * P, (pair + 1) * P)
-                    nc.tensor.matmul_mx(
-                        out=acc[(a, g)][:],
-                        lhsT=w_codes[:, m_cols].bitcast(FP8X4),
-                        lhsT_scale=w_scales[:, m_cols],
-                        rhs=x_codes[:, c, n_cols].bitcast(FP8X4),
-                        rhs_scale=x_scales[:, c, n_cols],
-                        start=(c == 0),
-                        stop=(c == PASSES - 1),
+        def multiply(c, pair):
+            if c == 0:
+                acc[pair] = psum.tile([P, P], F32, name="acc", tag="bank")
+            a, g = pair // 2, pair % 2
+            w_codes, w_scales = w_operand[(a, c)]
+            x_codes, x_scales = x_operand[c]
+            m_cols = slice(g * P, (g + 1) * P)
+            n_cols = slice(pair * P, (pair + 1) * P)
+            nc.tensor.matmul_mx(
+                out=acc[pair][:],
+                lhsT=w_codes[:, m_cols].bitcast(FP8X4),
+                lhsT_scale=w_scales[:, m_cols],
+                rhs=x_codes[:, n_cols].bitcast(FP8X4),
+                rhs_scale=x_scales[:, n_cols],
+                start=(c == 0),
+                stop=(c == PASSES - 1),
+            )
+
+        def add_bias(pair, on_scalar):
+            l, i = pair // 4, pair % 4
+            sums = result[l][:, i].rearrange("p n z w -> p (n z w)")
+            bias = bias_sb[:, pair : pair + 1]
+            if on_scalar:
+                nc.scalar.activation(out=sums, in_=acc[pair][:], func=IDENTITY, bias=bias)
+            else:
+                nc.vector.tensor_scalar_add(out=sums, in0=acc[pair][:], scalar1=bias)
+
+        def store(l):
+            for z in range(2):
+                rows = slice(z * OUT_CH, (z + 1) * OUT_CH)
+                copy = nc.vector.tensor_copy if z == 0 else nc.scalar.copy
+                copy(
+                    out=out_sb[l][rows].rearrange("p n (w i) -> p n w i", i=4),
+                    in_=result[l][rows, :, :, z, :].rearrange("p i n w -> p n w i"),
+                )
+                for b in range(BATCH):
+                    queue = nc.sync if b == 0 else nc.scalar
+                    queue.dma_start(
+                        out=out[b].rearrange("o (h l z) c -> l z o h c", l=2, z=2)[l, z],
+                        in_=out_sb[l][rows, 4 * b : 4 * b + 4],
                     )
 
-        def add_bias(q):
-            if not 0 <= q < len(pieces):
-                return
-            a, first, passes = pieces[q]
-            if first + passes < PASSES:
-                return
-            for g in range(2):
-                l, i = a // 2, 2 * (a % 2) + g
-                nc.vector.tensor_scalar_add(
-                    out=result[:, l, i].rearrange("p n z w -> p (n z w)"),
-                    in0=acc[(a, g)][:],
-                    scalar1=bias_sb[:, 4 * l + i : 4 * l + i + 1],
-                )
-
+        last = PASSES - 1
+        multiplied = 0
+        quantised = 0
         with tc.manual_schedule():
-            for c in range(PASSES + 1):
-                if c < PASSES:
-                    load_x(c)
-                    regroup_x(c)
-                if c >= 1:
-                    quantise_x(c - 1)
-            for q in range(len(pieces) + 2):
-                if q < len(pieces):
-                    load_w(q)
-                if 0 <= q - 1 < len(pieces):
-                    quantise_w(q - 1)
-                if q < len(pieces):
-                    transpose_w(q)
-                if 0 <= q - 1 < len(pieces):
-                    multiply(q - 1)
-                add_bias(q - 2)
-
-        for z in range(2):
-            rows = slice(z * OUT_CH, (z + 1) * OUT_CH)
-            copy = nc.vector.tensor_copy if z == 0 else nc.scalar.copy
+            for s in range(len(units) + 1):
+                if s < len(units):
+                    kind, index = units[s]
+                    if kind == "w":
+                        load_w(index)
+                        transpose_w(index)
+                    else:
+                        load_x(index)
+                        if index == last:
+                            regroup_x(index, on_scalar=[(0, 1), (1, 1)])
+                        elif index == 0 or index >= EARLY:
+                            regroup_x(index, on_scalar=[(1, 0), (1, 1)])
+                        else:
+                            regroup_x(index, on_scalar=[(1, 1)])
+                if s == 1:
+                    nc.vector.memset(bias_rows[:], 0.0)
+                    nc.vector.tensor_copy(out=bias_rows[0:PAIRS, :], in_=bg_sb[:])
+                    bias_ps = psum.tile([P, 4 * P], F32, name="bias_ps", tag="bank")
+                    nc.tensor.transpose(bias_ps[:, 0:P], bias_rows[:], ident[:])
+                    nc.vector.tensor_copy(out=bias_sb[:], in_=bias_ps[:, 0:PAIRS])
+                if s > 0:
+                    kind, index = units[s - 1]
+                    if kind == "w":
+                        quantise_w(index)
+                    else:
+                        quantise_x(index, halves=2 if index == last else 1)
+                        quantised += 1
+                    if len(w_operand) == 4 * PASSES:
+                        while multiplied < min(quantised, last):
+                            for pair in range(PAIRS):
+                                multiply(multiplied, pair)
+                            multiplied += 1
             for l in range(2):
-                copy(
-                    out=out_sb[rows, :].rearrange("p (n l w i) -> p l n w i", l=2, w=8, i=4)[:, l],
-                    in_=result[rows, l, :, :, z, :].rearrange("p i n w -> p n w i"),
-                )
-            for b in range(BATCH):
-                queue = nc.sync if b == 0 else nc.scalar
-                queue.dma_start(
-                    out=out[b].rearrange("o (m z) c -> z o m c", z=2)[z],
-                    in_=out_sb[rows, b * 256 : (b + 1) * 256].rearrange("p (m c) -> p m c", c=COLS),
-                )
+                for i in range(4):
+                    multiply(last, 4 * l + i)
+                for i in range(4):
+                    add_bias(4 * l + i, on_scalar=(l == 0 or i % 2 == 1))
+                store(l)

@@ -20,7 +20,7 @@ PASSES = CHANNELS // K_PASS
 PIECE = 4
 PIECES = 4 * (PASSES // PIECE)
 PAIRS = 8
-EARLY = 10
+EARLY = 13
 
 
 def tile_groupwiselinearprojector_k_kernel(tc, x, Wg, bg, out):
@@ -32,8 +32,9 @@ def tile_groupwiselinearprojector_k_kernel(tc, x, Wg, bg, out):
         tc.tile_pool(name="raw", bufs=6) as raw,
         tc.tile_pool(name="grouped", bufs=4) as grouped,
         tc.tile_pool(name="w_ops", bufs=PIECES) as w_ops,
-        tc.tile_pool(name="x_ops", bufs=EARLY + 3) as x_ops,
-        tc.psum_pool(name="psum", bufs=8) as psum,
+        tc.tile_pool(name="x_ops", bufs=EARLY + 1) as x_ops,
+        tc.psum_pool(name="psum_t", bufs=4) as psum_t,
+        tc.psum_pool(name="psum_acc", bufs=4) as psum_acc,
     ):
         ident = consts.tile([P, P], F32)
         make_identity(nc, ident[:])
@@ -112,7 +113,7 @@ def tile_groupwiselinearprojector_k_kernel(tc, x, Wg, bg, out):
                 "p (c g z o u) -> p c g z o u", c=PIECE, g=2, z=2, o=OUT_CH
             )
             for c in range(PIECE):
-                wt = psum.tile([P, 2, 2, P], F32, name="wt", tag="bank")
+                wt = psum_t.tile([P, 2, 2, P], F32, name="wt", tag="wt")
                 for z in range(2):
                     for u in range(2):
                         nc.tensor.transpose(wt[:, z, u, :], raw_words[:, z, c, :, u], ident[:])
@@ -133,7 +134,10 @@ def tile_groupwiselinearprojector_k_kernel(tc, x, Wg, bg, out):
 
         def multiply(c, pair):
             if c == 0:
-                acc[pair] = psum.tile([P, P], F32, name="acc", tag="bank")
+                if pair < 4:
+                    acc[pair] = psum_acc.tile([P, P], F32, name="acc", tag="acc")
+                else:
+                    acc[pair] = psum_t.tile([P, P], F32, name="acc", tag="wt")
             a, g = pair // 2, pair % 2
             w_codes, w_scales = w_operand[(a, c)]
             x_codes, x_scales = x_operand[c]
@@ -161,57 +165,72 @@ def tile_groupwiselinearprojector_k_kernel(tc, x, Wg, bg, out):
         def store(l):
             for z in range(2):
                 rows = slice(z * OUT_CH, (z + 1) * OUT_CH)
-                copy = nc.vector.tensor_copy if z == 0 else nc.scalar.copy
+                copy = nc.vector.tensor_copy if (l, z) == (1, 0) else nc.scalar.copy
                 copy(
                     out=out_sb[l][rows].rearrange("p n (w i) -> p n w i", i=4),
                     in_=result[l][rows, :, :, z, :].rearrange("p i n w -> p n w i"),
                 )
                 for b in range(BATCH):
-                    queue = nc.sync if b == 0 else nc.scalar
+                    queue = nc.sync if z == 0 else nc.scalar
                     queue.dma_start(
                         out=out[b].rearrange("o (h l z) c -> l z o h c", l=2, z=2)[l, z],
                         in_=out_sb[l][rows, 4 * b : 4 * b + 4],
                     )
 
         last = PASSES - 1
-        multiplied = 0
-        quantised = 0
+        x_ready = 0
+        next_pass = [0] * PAIRS
+
+        def multiply_ready(pairs, passes):
+            for c in range(passes):
+                for pair in pairs:
+                    if next_pass[pair] == c and (pair // 2, c) in w_operand:
+                        multiply(c, pair)
+                        next_pass[pair] += 1
+
         with tc.manual_schedule():
             for s in range(len(units) + 1):
-                if s < len(units):
-                    kind, index = units[s]
-                    if kind == "w":
-                        load_w(index)
-                        transpose_w(index)
+                ready_before = x_ready
+                kind, index = units[min(s, len(units) - 1)]
+                if s == len(units):
+                    pass
+                elif kind == "w":
+                    load_w(index)
+                    transpose_w(index)
+                else:
+                    load_x(index)
+                    if index == last:
+                        quantise_x(last - 1, halves=1)
+                        x_ready += 1
+                        regroup_x(index, on_scalar=[(0, 1), (1, 1)])
+                    elif index == 0 or index >= EARLY:
+                        regroup_x(index, on_scalar=[(1, 0), (1, 1)])
                     else:
-                        load_x(index)
-                        if index == last:
-                            regroup_x(index, on_scalar=[(0, 1), (1, 1)])
-                        elif index == 0 or index >= EARLY:
-                            regroup_x(index, on_scalar=[(1, 0), (1, 1)])
-                        else:
-                            regroup_x(index, on_scalar=[(1, 1)])
+                        regroup_x(index, on_scalar=[(1, 1)])
                 if s == 1:
                     nc.vector.memset(bias_rows[:], 0.0)
                     nc.vector.tensor_copy(out=bias_rows[0:PAIRS, :], in_=bg_sb[:])
-                    bias_ps = psum.tile([P, 4 * P], F32, name="bias_ps", tag="bank")
-                    nc.tensor.transpose(bias_ps[:, 0:P], bias_rows[:], ident[:])
+                elif s == 3:
+                    bias_ps = psum_acc.tile([P, P], F32, name="bias_ps", tag="acc")
+                    nc.tensor.transpose(bias_ps[:], bias_rows[:], ident[:])
+                elif s == 5:
                     nc.vector.tensor_copy(out=bias_sb[:], in_=bias_ps[:, 0:PAIRS])
-                if s > 0:
-                    kind, index = units[s - 1]
-                    if kind == "w":
+                for lag in (2, 1):
+                    if not 0 <= s - lag < len(units):
+                        continue
+                    done, index = units[s - lag]
+                    if done == "w" and lag == 2:
                         quantise_w(index)
-                    else:
+                    elif done == "x" and lag == 1 and index != last - 1:
                         quantise_x(index, halves=2 if index == last else 1)
-                        quantised += 1
-                    if len(w_operand) == 4 * PASSES:
-                        while multiplied < min(quantised, last):
-                            for pair in range(PAIRS):
-                                multiply(multiplied, pair)
-                            multiplied += 1
+                        x_ready += 1
+                if len(w_operand) == 4 * PASSES:
+                    multiply_ready(range(PAIRS), min(x_ready, last))
+                elif len(w_operand) >= 2 * PASSES:
+                    multiply_ready(range(4), ready_before)
             for l in range(2):
                 for i in range(4):
                     multiply(last, 4 * l + i)
                 for i in range(4):
-                    add_bias(4 * l + i, on_scalar=(l == 0 or i % 2 == 1))
+                    add_bias(4 * l + i, on_scalar=(l == 0))
                 store(l)

@@ -52,18 +52,17 @@ def tile_groupwiselinearprojector_k_kernel(tc, x, Wg, bg, out):
         out_sb = [consts.tile([P, 8, COLS], F32, name=f"out_sb_{l}") for l in range(2)]
 
         raw_x, grouped_x, x_operand = {}, {}, {}
-        raw_w, grouped_w = {}, {}
+        raw_w = {}
+        grouped_w = {}
         w_operand = {}
         acc = {}
 
-        units = []
-        early = 0
+        units = [("x", 0), ("x", 1)]
+        spread = EARLY - 2
         for q in range(PIECES):
-            while early * PIECES <= q * EARLY and early < EARLY:
-                units.append(("x", early))
-                early += 1
             units.append(("w", q))
-        units += [("x", c) for c in range(early, PASSES)]
+            units += [("x", 2 + n) for n in range(q * spread // PIECES, (q + 1) * spread // PIECES)]
+        units += [("x", c) for c in range(EARLY, PASSES)]
 
         def load_x(c):
             raw_x[c] = raw.tile([P, BATCH, PACK, PIXELS], BF16, name="raw_x", tag="raw")
@@ -99,15 +98,20 @@ def tile_groupwiselinearprojector_k_kernel(tc, x, Wg, bg, out):
                 )
 
         def load_w(q):
-            a, first = q // 4, PIECE * (q % 4)
-            raw_w[q] = raw.tile([P, 2 * PIECE * K_PASS], BF16, name="raw_w", tag="raw")
-            nc.sync.dma_start(
-                out=raw_w[q][:].rearrange("p (z k) -> p z k", z=2),
-                in_=w_rows[a // 2, a % 2][:, :, first * K_PASS : (first + PIECE) * K_PASS],
-            )
+            a, half = q // 4, q % 4 // 2
+            channels = 2 * PIECE * K_PASS
+            for z in range(2):
+                raw_w[(q // 2, z)] = raw.tile([P, channels], BF16, name="raw_w", tag="raw")
+                nc.sync.dma_start(
+                    out=raw_w[(q // 2, z)][:],
+                    in_=w_rows[a // 2, a % 2][:, z, half * channels : (half + 1) * channels],
+                )
 
         def transpose_w(q):
-            raw_words = raw_w[q][:].bitcast(F32).rearrange("p (z c q u) -> p z c q u", z=2, c=PIECE, u=2)
+            raw_words = [
+                raw_w[(q // 2, z)][:].bitcast(F32).rearrange("p (c q u) -> p c q u", c=2 * PIECE, u=2) for z in range(2)
+            ]
+            offset = PIECE * (q % 2)
             grouped_w[q] = grouped.tile([P, PIECE * 2 * P * PACK], BF16, align_bytes=64, name="grouped_w", tag="grouped")
             grouped_words = grouped_w[q][:].bitcast(F32).rearrange(
                 "p (c g z o u) -> p c g z o u", c=PIECE, g=2, z=2, o=OUT_CH
@@ -116,7 +120,7 @@ def tile_groupwiselinearprojector_k_kernel(tc, x, Wg, bg, out):
                 wt = psum_t.tile([P, 2, 2, P], F32, name="wt", tag="wt")
                 for z in range(2):
                     for u in range(2):
-                        nc.tensor.transpose(wt[:, z, u, :], raw_words[:, z, c, :, u], ident[:])
+                        nc.tensor.transpose(wt[:, z, u, :], raw_words[z][:, offset + c, :, u], ident[:])
                 for z in range(2):
                     nc.scalar.copy(
                         out=grouped_words[:, c, :, z, :, :],
@@ -195,7 +199,8 @@ def tile_groupwiselinearprojector_k_kernel(tc, x, Wg, bg, out):
                 if s == len(units):
                     pass
                 elif kind == "w":
-                    load_w(index)
+                    if index % 2 == 0:
+                        load_w(index)
                     transpose_w(index)
                 else:
                     load_x(index)
@@ -203,7 +208,7 @@ def tile_groupwiselinearprojector_k_kernel(tc, x, Wg, bg, out):
                         quantise_x(last - 1, halves=1)
                         x_ready += 1
                         regroup_x(index, on_scalar=[(0, 1), (1, 1)])
-                    elif index == 0 or index >= EARLY:
+                    elif index <= 1 or index >= EARLY:
                         regroup_x(index, on_scalar=[(1, 0), (1, 1)])
                     else:
                         regroup_x(index, on_scalar=[(1, 1)])

@@ -78,11 +78,8 @@ def tile_groupwiselinearprojector_k_kernel(tc, x, Wg, bg, out):
             dst = grouped_x[c][:].rearrange("p l i (b h m) t -> p b l h m t i", b=BATCH, h=4)
             for b in range(BATCH):
                 for l in range(2):
-                    if (b, l) in on_scalar:
-                        for h in range(4):
-                            nc.scalar.copy(out=dst[:, b, l, h], in_=src[:, b, l, h])
-                    else:
-                        nc.vector.tensor_copy(out=dst[:, b, l], in_=src[:, b, l])
+                    copy = nc.scalar.copy if (b, l) in on_scalar else nc.vector.tensor_copy
+                    copy(out=dst[:, b, l], in_=src[:, b, l])
 
         def quantise_x(c, halves):
             x_codes = x_ops.tile([P, PAIRS * P], U32, align_bytes=64)
@@ -121,11 +118,10 @@ def tile_groupwiselinearprojector_k_kernel(tc, x, Wg, bg, out):
                 for z in range(2):
                     for u in range(2):
                         nc.tensor.transpose(wt[:, z, u, :], raw_words[z][:, offset + c, :, u], ident[:])
-                for z in range(2):
-                    nc.scalar.copy(
-                        out=grouped_words[:, c, :, z, :, :],
-                        in_=wt[:, z].rearrange("p u (g o) -> p g o u", g=2),
-                    )
+                nc.scalar.copy(
+                    out=grouped_words[:, c],
+                    in_=wt[:].rearrange("p z u (g o) -> p g z o u", g=2),
+                )
 
         def quantise_w(q):
             a, first = q // 4, PIECE * (q % 4)

@@ -65,7 +65,7 @@ def tile_groupwiselinearprojector_k_kernel(tc, x, Wg, bg, out):
         units += [("x", c) for c in range(EARLY, PASSES)]
 
         def load_x(c):
-            raw_x[c] = raw.tile([P, BATCH, PACK, PIXELS], BF16, name="raw_x", tag="raw")
+            raw_x[c] = raw.tile([P, BATCH, PACK, PIXELS], BF16, align_bytes=256, name="raw_x", tag="raw")
             for b in range(BATCH):
                 nc.sync.dma_start(
                     out=raw_x[c][:, b].rearrange("p t x -> p (t x)"),
@@ -98,7 +98,7 @@ def tile_groupwiselinearprojector_k_kernel(tc, x, Wg, bg, out):
             a, half = q // 4, q % 4 // 2
             channels = 2 * PIECE * K_PASS
             for z in range(2):
-                raw_w[(q // 2, z)] = raw.tile([P, channels], BF16, name="raw_w", tag="raw")
+                raw_w[(q // 2, z)] = raw.tile([P, channels], BF16, align_bytes=256, name="raw_w", tag="raw")
                 nc.sync.dma_start(
                     out=raw_w[(q // 2, z)][:],
                     in_=w_rows[a // 2, a % 2][:, z, half * channels : (half + 1) * channels],

@@ -20,7 +20,13 @@ PASSES = CHANNELS // K_PASS
 PIECE = 4
 PIECES = 4 * (PASSES // PIECE)
 PAIRS = 8
-EARLY = 13
+LEAD = 2
+WLAG = 1
+RAW = 6
+MIDS = [(1, 1)]
+LATE = [(1, 0), (1, 1)]
+ENDS = [(0, 1), (1, 1)]
+EARLY = 11
 
 
 def tile_groupwiselinearprojector_k_kernel(tc, x, Wg, bg, out):
@@ -29,12 +35,11 @@ def tile_groupwiselinearprojector_k_kernel(tc, x, Wg, bg, out):
 
     with (
         tc.tile_pool(name="consts", bufs=1) as consts,
-        tc.tile_pool(name="raw", bufs=6) as raw,
+        tc.tile_pool(name="raw", bufs=RAW) as raw,
         tc.tile_pool(name="grouped", bufs=4) as grouped,
         tc.tile_pool(name="w_ops", bufs=PIECES) as w_ops,
         tc.tile_pool(name="x_ops", bufs=EARLY + 1) as x_ops,
-        tc.psum_pool(name="psum_t", bufs=4) as psum_t,
-        tc.psum_pool(name="psum_acc", bufs=4) as psum_acc,
+        tc.psum_pool(name="psum", bufs=8) as psum,
     ):
         ident = consts.tile([P, P], F32)
         make_identity(nc, ident[:])
@@ -57,11 +62,12 @@ def tile_groupwiselinearprojector_k_kernel(tc, x, Wg, bg, out):
         w_operand = {}
         acc = {}
 
-        units = [("x", 0), ("x", 1)]
-        spread = EARLY - 2
+        units = [("x", c) for c in range(LEAD)]
+        spread = EARLY - LEAD
         for q in range(PIECES):
             units.append(("w", q))
-            units += [("x", 2 + n) for n in range(q * spread // PIECES, (q + 1) * spread // PIECES)]
+            n0, n1 = (min(n * spread // PIECES, spread) for n in (q, q + 1))
+            units += [("x", LEAD + n) for n in range(n0, n1)]
         units += [("x", c) for c in range(EARLY, PASSES)]
 
         def load_x(c):
@@ -114,7 +120,7 @@ def tile_groupwiselinearprojector_k_kernel(tc, x, Wg, bg, out):
                 "p (c g z o u) -> p c g z o u", c=PIECE, g=2, z=2, o=OUT_CH
             )
             for c in range(PIECE):
-                wt = psum_t.tile([P, 2, 2, P], F32, name="wt", tag="wt")
+                wt = psum.tile([P, 2, 2, P], F32, name="wt", tag="bank")
                 for z in range(2):
                     for u in range(2):
                         nc.tensor.transpose(wt[:, z, u, :], raw_words[z][:, offset + c, :, u], ident[:])
@@ -134,10 +140,7 @@ def tile_groupwiselinearprojector_k_kernel(tc, x, Wg, bg, out):
 
         def multiply(c, pair):
             if c == 0:
-                if pair < 4:
-                    acc[pair] = psum_acc.tile([P, P], F32, name="acc", tag="acc")
-                else:
-                    acc[pair] = psum_t.tile([P, P], F32, name="acc", tag="wt")
+                acc[pair] = psum.tile([P, P], F32, name="acc", tag="bank")
             a, g = pair // 2, pair % 2
             w_codes, w_scales = w_operand[(a, c)]
             x_codes, x_scales = x_operand[c]
@@ -203,16 +206,16 @@ def tile_groupwiselinearprojector_k_kernel(tc, x, Wg, bg, out):
                     if index == last:
                         quantise_x(last - 1, halves=1)
                         x_ready += 1
-                        regroup_x(index, on_scalar=[(0, 1), (1, 1)])
-                    elif index <= 1 or index >= EARLY:
-                        regroup_x(index, on_scalar=[(1, 0), (1, 1)])
+                        regroup_x(index, on_scalar=ENDS)
+                    elif index < LEAD or index >= EARLY:
+                        regroup_x(index, on_scalar=LATE)
                     else:
-                        regroup_x(index, on_scalar=[(1, 1)])
+                        regroup_x(index, on_scalar=MIDS)
                 if s == 1:
                     nc.vector.memset(bias_rows[:], 0.0)
                     nc.vector.tensor_copy(out=bias_rows[0:PAIRS, :], in_=bg_sb[:])
                 elif s == 3:
-                    bias_ps = psum_acc.tile([P, P], F32, name="bias_ps", tag="acc")
+                    bias_ps = psum.tile([P, P], F32, name="bias_ps", tag="bank")
                     nc.tensor.transpose(bias_ps[:], bias_rows[:], ident[:])
                 elif s == 5:
                     nc.vector.tensor_copy(out=bias_sb[:], in_=bias_ps[:, 0:PAIRS])
@@ -220,15 +223,13 @@ def tile_groupwiselinearprojector_k_kernel(tc, x, Wg, bg, out):
                     if not 0 <= s - lag < len(units):
                         continue
                     done, index = units[s - lag]
-                    if done == "w" and lag == 2:
+                    if done == "w" and lag == WLAG:
                         quantise_w(index)
                     elif done == "x" and lag == 1 and index != last - 1:
                         quantise_x(index, halves=2 if index == last else 1)
                         x_ready += 1
                 if len(w_operand) == 4 * PASSES:
                     multiply_ready(range(PAIRS), min(x_ready, last))
-                elif len(w_operand) >= 2 * PASSES:
-                    multiply_ready(range(4), ready_before)
             for l in range(2):
                 for i in range(4):
                     multiply(last, 4 * l + i)

@@ -17,16 +17,19 @@ K_PASS = P * PACK
 BATCH, CHANNELS, OUT_CH, ROWS, COLS = 2, 8192, 64, 16, 32
 PIXELS = ROWS * COLS
 PASSES = CHANNELS // K_PASS
-PIECE = 4
-PIECES = 4 * (PASSES // PIECE)
+LAST = PASSES - 1
+
 PAIRS = 8
+QUADS = 4
+
+PIECE = 4
+PIECES = QUADS * (PASSES // PIECE)
+ALONE = PIECES // 2
+
 LEAD = 2
-WLAG = 1
-RAW = 6
-MIDS = [(1, 1)]
-LATE = [(1, 0), (1, 1)]
-ENDS = [(0, 1), (1, 1)]
-EARLY = 11
+EARLY = 12
+
+LOAD_ALIGN = 256
 
 
 def tile_groupwiselinearprojector_k_kernel(tc, x, Wg, bg, out):
@@ -35,11 +38,11 @@ def tile_groupwiselinearprojector_k_kernel(tc, x, Wg, bg, out):
 
     with (
         tc.tile_pool(name="consts", bufs=1) as consts,
-        tc.tile_pool(name="raw", bufs=RAW) as raw,
+        tc.tile_pool(name="raw", bufs=6) as raw,
         tc.tile_pool(name="grouped", bufs=4) as grouped,
         tc.tile_pool(name="w_ops", bufs=PIECES) as w_ops,
         tc.tile_pool(name="x_ops", bufs=EARLY + 1) as x_ops,
-        tc.psum_pool(name="psum", bufs=8) as psum,
+        tc.psum_pool(name="psum", bufs=PAIRS) as psum,
     ):
         ident = consts.tile([P, P], F32)
         make_identity(nc, ident[:])
@@ -57,21 +60,19 @@ def tile_groupwiselinearprojector_k_kernel(tc, x, Wg, bg, out):
         out_sb = [consts.tile([P, 8, COLS], F32, name=f"out_sb_{l}") for l in range(2)]
 
         raw_x, grouped_x, x_operand = {}, {}, {}
-        raw_w = {}
+        raw_w, w_operand = {}, {}
         grouped_w = {}
-        w_operand = {}
-        acc = {}
+        sums = {}
 
         units = [("x", c) for c in range(LEAD)]
         spread = EARLY - LEAD
         for q in range(PIECES):
             units.append(("w", q))
-            n0, n1 = (min(n * spread // PIECES, spread) for n in (q, q + 1))
-            units += [("x", LEAD + n) for n in range(n0, n1)]
+            units += [("x", LEAD + n) for n in range(q * spread // PIECES, (q + 1) * spread // PIECES)]
         units += [("x", c) for c in range(EARLY, PASSES)]
 
         def load_x(c):
-            raw_x[c] = raw.tile([P, BATCH, PACK, PIXELS], BF16, align_bytes=256, name="raw_x", tag="raw")
+            raw_x[c] = raw.tile([P, BATCH, PACK, PIXELS], BF16, align_bytes=LOAD_ALIGN, name="raw_x", tag="raw")
             for b in range(BATCH):
                 nc.sync.dma_start(
                     out=raw_x[c][:, b].rearrange("p t x -> p (t x)"),
@@ -87,46 +88,55 @@ def tile_groupwiselinearprojector_k_kernel(tc, x, Wg, bg, out):
                     copy = nc.scalar.copy if (b, l) in on_scalar else nc.vector.tensor_copy
                     copy(out=dst[:, b, l], in_=src[:, b, l])
 
-        def quantise_x(c, halves):
+        def quantise_x(c, parts):
             x_codes = x_ops.tile([P, PAIRS * P], U32, align_bytes=64)
             x_scales = x_ops.tile([P, PAIRS * P], U8, align_bytes=64)
             x_operand[c] = (x_codes, x_scales)
-            flat = grouped_x[c][:].rearrange("p l i m t -> p (l i m t)")
-            cols = PAIRS * P // halves
-            for half in range(halves):
+            values = grouped_x[c][:].rearrange("p l i m t -> p (l i m t)")
+            width = PAIRS * P // parts
+            for part in range(parts):
+                cols = slice(part * width, (part + 1) * width)
                 nc.vector.quantize_mx(
-                    out=x_codes[:, half * cols : (half + 1) * cols].bitcast(FP8X4),
-                    scales=x_scales[:, half * cols : (half + 1) * cols],
-                    in_=flat[:, half * cols * PACK : (half + 1) * cols * PACK],
+                    out=x_codes[:, cols].bitcast(FP8X4),
+                    scales=x_scales[:, cols],
+                    in_=values[:, part * width * PACK : (part + 1) * width * PACK],
                 )
 
         def load_w(q):
-            a, half = q // 4, q % 4 // 2
-            channels = 2 * PIECE * K_PASS
-            for z in range(2):
-                raw_w[(q // 2, z)] = raw.tile([P, channels], BF16, align_bytes=256, name="raw_w", tag="raw")
-                nc.sync.dma_start(
-                    out=raw_w[(q // 2, z)][:],
-                    in_=w_rows[a // 2, a % 2][:, z, half * channels : (half + 1) * channels],
-                )
+            a, first = q // 4, PIECE * (q % 4)
+            source = w_rows[a // 2, a % 2]
+            if q >= PIECES - ALONE:
+                channels = PIECE * K_PASS
+                tile = raw.tile([P, 2, channels], BF16, align_bytes=LOAD_ALIGN, name="raw_w", tag="raw")
+                nc.sync.dma_start(out=tile[:], in_=source[:, :, first * K_PASS : first * K_PASS + channels])
+                halves = [tile[:, z] for z in range(2)]
+            elif q % 2 == 0:
+                channels = 2 * PIECE * K_PASS
+                halves = []
+                for z in range(2):
+                    tile = raw.tile([P, channels], BF16, align_bytes=LOAD_ALIGN, name="raw_w", tag="raw")
+                    nc.sync.dma_start(out=tile[:], in_=source[:, z, first * K_PASS : first * K_PASS + channels])
+                    halves.append(tile[:])
+            else:
+                return
+            for c in range(channels // K_PASS):
+                raw_w[(a, first + c)] = [half[:, c * K_PASS : (c + 1) * K_PASS] for half in halves]
 
         def transpose_w(q):
-            raw_words = [
-                raw_w[(q // 2, z)][:].bitcast(F32).rearrange("p (c q u) -> p c q u", c=2 * PIECE, u=2) for z in range(2)
-            ]
-            offset = PIECE * (q % 2)
+            a, first = q // 4, PIECE * (q % 4)
             grouped_w[q] = grouped.tile([P, PIECE * 2 * P * PACK], BF16, align_bytes=64, name="grouped_w", tag="grouped")
             grouped_words = grouped_w[q][:].bitcast(F32).rearrange(
                 "p (c g z o u) -> p c g z o u", c=PIECE, g=2, z=2, o=OUT_CH
             )
             for c in range(PIECE):
-                wt = psum.tile([P, 2, 2, P], F32, name="wt", tag="bank")
+                bank = psum.tile([P, 2, 2, P], F32, name="transposed", tag="bank")
                 for z in range(2):
+                    words = raw_w[(a, first + c)][z].bitcast(F32).rearrange("p (q u) -> p q u", u=2)
                     for u in range(2):
-                        nc.tensor.transpose(wt[:, z, u, :], raw_words[z][:, offset + c, :, u], ident[:])
+                        nc.tensor.transpose(bank[:, z, u, :], words[:, :, u], ident[:])
                 nc.scalar.copy(
                     out=grouped_words[:, c],
-                    in_=wt[:].rearrange("p z u (g o) -> p g z o u", g=2),
+                    in_=bank[:].rearrange("p z u (g o) -> p g z o u", g=2),
                 )
 
         def quantise_w(q):
@@ -140,77 +150,63 @@ def tile_groupwiselinearprojector_k_kernel(tc, x, Wg, bg, out):
 
         def multiply(c, pair):
             if c == 0:
-                acc[pair] = psum.tile([P, P], F32, name="acc", tag="bank")
-            a, g = pair // 2, pair % 2
+                sums[pair] = psum.tile([P, P], F32, name="sums", tag="bank")
+            a, g2 = pair // 2, pair % 2
             w_codes, w_scales = w_operand[(a, c)]
             x_codes, x_scales = x_operand[c]
-            m_cols = slice(g * P, (g + 1) * P)
+            m_cols = slice(g2 * P, (g2 + 1) * P)
             n_cols = slice(pair * P, (pair + 1) * P)
             nc.tensor.matmul_mx(
-                out=acc[pair][:],
+                out=sums[pair][:],
                 lhsT=w_codes[:, m_cols].bitcast(FP8X4),
                 lhsT_scale=w_scales[:, m_cols],
                 rhs=x_codes[:, n_cols].bitcast(FP8X4),
                 rhs_scale=x_scales[:, n_cols],
                 start=(c == 0),
-                stop=(c == PASSES - 1),
+                stop=(c == LAST),
             )
 
-        def add_bias(pair, on_scalar):
+        def add_bias(pair):
             l, i = pair // 4, pair % 4
-            sums = result[l][:, i].rearrange("p n z w -> p (n z w)")
+            to = result[l][:, i].rearrange("p n z w -> p (n z w)")
             bias = bias_sb[:, pair : pair + 1]
-            if on_scalar:
-                nc.scalar.activation(out=sums, in_=acc[pair][:], func=IDENTITY, bias=bias)
+            if l == 0:
+                nc.scalar.activation(out=to, in_=sums[pair][:], func=IDENTITY, bias=bias)
             else:
-                nc.vector.tensor_scalar_add(out=sums, in0=acc[pair][:], scalar1=bias)
+                nc.vector.tensor_scalar_add(out=to, in0=sums[pair][:], scalar1=bias)
 
         def store(l):
+            copy = nc.scalar.copy if l == 0 else nc.vector.tensor_copy
             for z in range(2):
                 rows = slice(z * OUT_CH, (z + 1) * OUT_CH)
-                copy = nc.vector.tensor_copy if (l, z) == (1, 0) else nc.scalar.copy
                 copy(
                     out=out_sb[l][rows].rearrange("p n (w i) -> p n w i", i=4),
                     in_=result[l][rows, :, :, z, :].rearrange("p i n w -> p n w i"),
                 )
+                queue = nc.sync if z == 0 else nc.scalar
                 for b in range(BATCH):
-                    queue = nc.sync if z == 0 else nc.scalar
                     queue.dma_start(
                         out=out[b].rearrange("o (h l z) c -> l z o h c", l=2, z=2)[l, z],
                         in_=out_sb[l][rows, 4 * b : 4 * b + 4],
                     )
 
-        last = PASSES - 1
-        x_ready = 0
-        next_pass = [0] * PAIRS
-
-        def multiply_ready(pairs, passes):
-            for c in range(passes):
-                for pair in pairs:
-                    if next_pass[pair] == c and (pair // 2, c) in w_operand:
-                        multiply(c, pair)
-                        next_pass[pair] += 1
-
         with tc.manual_schedule():
+            multiplied = 0
             for s in range(len(units) + 1):
-                ready_before = x_ready
-                kind, index = units[min(s, len(units) - 1)]
-                if s == len(units):
-                    pass
-                elif kind == "w":
-                    if index % 2 == 0:
+                if s < len(units):
+                    kind, index = units[s]
+                    if kind == "w":
                         load_w(index)
-                    transpose_w(index)
-                else:
-                    load_x(index)
-                    if index == last:
-                        quantise_x(last - 1, halves=1)
-                        x_ready += 1
-                        regroup_x(index, on_scalar=ENDS)
-                    elif index < LEAD or index >= EARLY:
-                        regroup_x(index, on_scalar=LATE)
+                        transpose_w(index)
                     else:
-                        regroup_x(index, on_scalar=MIDS)
+                        load_x(index)
+                        if index == LAST:
+                            on_scalar = [(0, 1), (1, 1)]
+                        elif LEAD <= index < EARLY:
+                            on_scalar = [(1, 1)]
+                        else:
+                            on_scalar = [(1, 0), (1, 1)]
+                        regroup_x(index, on_scalar)
                 if s == 1:
                     nc.vector.memset(bias_rows[:], 0.0)
                     nc.vector.tensor_copy(out=bias_rows[0:PAIRS, :], in_=bg_sb[:])
@@ -219,20 +215,19 @@ def tile_groupwiselinearprojector_k_kernel(tc, x, Wg, bg, out):
                     nc.tensor.transpose(bias_ps[:], bias_rows[:], ident[:])
                 elif s == 5:
                     nc.vector.tensor_copy(out=bias_sb[:], in_=bias_ps[:, 0:PAIRS])
-                for lag in (2, 1):
-                    if not 0 <= s - lag < len(units):
-                        continue
-                    done, index = units[s - lag]
-                    if done == "w" and lag == WLAG:
-                        quantise_w(index)
-                    elif done == "x" and lag == 1 and index != last - 1:
-                        quantise_x(index, halves=2 if index == last else 1)
-                        x_ready += 1
-                if len(w_operand) == 4 * PASSES:
-                    multiply_ready(range(PAIRS), min(x_ready, last))
+                if s >= 2 and units[s - 2][0] == "w":
+                    quantise_w(units[s - 2][1])
+                if s >= 1 and units[s - 1][0] == "x":
+                    c = units[s - 1][1]
+                    quantise_x(c, parts=2 if c == LAST else 1)
+                if len(w_operand) == QUADS * PASSES:
+                    for c in range(multiplied, min(len(x_operand), LAST)):
+                        for pair in range(PAIRS):
+                            multiply(c, pair)
+                        multiplied = c + 1
             for l in range(2):
                 for i in range(4):
-                    multiply(last, 4 * l + i)
+                    multiply(LAST, 4 * l + i)
                 for i in range(4):
-                    add_bias(4 * l + i, on_scalar=(l == 0))
+                    add_bias(4 * l + i)
                 store(l)

@@ -34,7 +34,7 @@ LOAD_ALIGN = 256
 
 def tile_groupwiselinearprojector_k_kernel(tc, x, Wg, bg, out):
     nc = tc.nc
-    w_rows = Wg.rearrange("g o k -> (g o) k").rearrange("(l z e p) k -> l e p z k", l=2, z=2, e=2)
+    w_rows = Wg.rearrange("g o k -> (g o) k").rearrange("(z l e p) k -> l e p z k", l=2, z=2, e=2)
 
     with (
         tc.tile_pool(name="consts", bufs=1) as consts,
@@ -51,13 +51,13 @@ def tile_groupwiselinearprojector_k_kernel(tc, x, Wg, bg, out):
         for l in range(2):
             nc.scalar.dma_start(
                 out=bg_sb[4 * l : 4 * l + 4, :].rearrange("i (z o) -> i z o", z=2),
-                in_=bg.rearrange("(l z i) o -> l i z o", l=2, z=2)[l],
+                in_=bg.rearrange("(z l i) o -> l i z o", l=2, z=2)[l],
             )
         bias_rows = consts.tile([P, P], F32)
         bias_sb = consts.tile([P, PAIRS], F32)
 
         result = [consts.tile([P, 4, 8, 2, 8], F32, name=f"result_{l}") for l in range(2)]
-        out_sb = [consts.tile([P, 8, COLS], F32, name=f"out_sb_{l}") for l in range(2)]
+        out_sb = consts.tile([P, 8, 2, COLS], F32)
 
         raw_x, grouped_x, x_operand = {}, {}, {}
         raw_w, w_operand = {}, {}
@@ -81,8 +81,8 @@ def tile_groupwiselinearprojector_k_kernel(tc, x, Wg, bg, out):
 
         def regroup_x(c, on_scalar):
             grouped_x[c] = grouped.tile([P, 2, 4, P, PACK], BF16, align_bytes=64, name="grouped_x", tag="grouped")
-            src = raw_x[c][:].rearrange("p b t (h l m i) -> p b l h m t i", h=4, l=2, i=4)
-            dst = grouped_x[c][:].rearrange("p l i (b h m) t -> p b l h m t i", b=BATCH, h=4)
+            src = raw_x[c][:].rearrange("p b t (a l w i) -> p b l a w t i", a=8, l=2, i=4)
+            dst = grouped_x[c][:].rearrange("p l i (b a w) t -> p b l a w t i", b=BATCH, a=8)
             for b in range(BATCH):
                 for l in range(2):
                     copy = nc.scalar.copy if (b, l) in on_scalar else nc.vector.tensor_copy
@@ -175,19 +175,23 @@ def tile_groupwiselinearprojector_k_kernel(tc, x, Wg, bg, out):
             else:
                 nc.vector.tensor_scalar_add(out=to, in0=sums[pair][:], scalar1=bias)
 
-        def store(l):
+        def gather(l):
             copy = nc.scalar.copy if l == 0 else nc.vector.tensor_copy
             for z in range(2):
                 rows = slice(z * OUT_CH, (z + 1) * OUT_CH)
                 copy(
-                    out=out_sb[l][rows].rearrange("p n (w i) -> p n w i", i=4),
+                    out=out_sb[rows, :, l, :].rearrange("p n (w i) -> p n w i", i=4),
                     in_=result[l][rows, :, :, z, :].rearrange("p i n w -> p n w i"),
                 )
+
+        def store():
+            for z in range(2):
+                rows = slice(z * OUT_CH, (z + 1) * OUT_CH)
                 queue = nc.sync if z == 0 else nc.scalar
                 for b in range(BATCH):
                     queue.dma_start(
-                        out=out[b].rearrange("o (h l z) c -> l z o h c", l=2, z=2)[l, z],
-                        in_=out_sb[l][rows, 4 * b : 4 * b + 4],
+                        out=out[b].rearrange("o (h z l) c -> z o h (l c)", l=2, z=2)[z],
+                        in_=out_sb[rows, 4 * b : 4 * b + 4].rearrange("p n l c -> p n (l c)"),
                     )
 
         with tc.manual_schedule():
@@ -230,4 +234,5 @@ def tile_groupwiselinearprojector_k_kernel(tc, x, Wg, bg, out):
                     multiply(LAST, 4 * l + i)
                 for i in range(4):
                     add_bias(4 * l + i)
-                store(l)
+                gather(l)
+            store()

@@ -8,7 +8,7 @@ BF16 = mybir.dt.bfloat16
 U32 = mybir.dt.uint32
 U8 = mybir.dt.uint8
 FP8X4 = mybir.dt.float8_e4m3fn_x4
-IDENTITY = mybir.ActivationFunctionType.Identity
+ADD = mybir.AluOpType.add
 
 P = 128
 PACK = 4
@@ -18,16 +18,16 @@ BATCH, CHANNELS, OUT_CH, ROWS, COLS = 2, 8192, 64, 16, 32
 PIXELS = ROWS * COLS
 PASSES = CHANNELS // K_PASS
 LAST = PASSES - 1
+HALF = PASSES // 2
 
 PAIRS = 8
 QUADS = 4
 
-PIECE = 4
-PIECES = QUADS * (PASSES // PIECE)
-ALONE = PIECES // 2
+PIECES = 2 * QUADS * 2
+PART = HALF // 2
 
 LEAD = 2
-EARLY = 12
+EARLY = 14
 
 LOAD_ALIGN = 256
 
@@ -38,11 +38,11 @@ def tile_groupwiselinearprojector_k_kernel(tc, x, Wg, bg, out):
 
     with (
         tc.tile_pool(name="consts", bufs=1) as consts,
-        tc.tile_pool(name="raw", bufs=6) as raw,
-        tc.tile_pool(name="grouped", bufs=4) as grouped,
-        tc.tile_pool(name="w_ops", bufs=PIECES) as w_ops,
-        tc.tile_pool(name="x_ops", bufs=EARLY + 1) as x_ops,
-        tc.psum_pool(name="psum", bufs=PAIRS) as psum,
+        tc.tile_pool(name="raw", bufs=7) as raw,
+        tc.tile_pool(name="grouped", bufs=6) as grouped,
+        tc.tile_pool(name="w_ops", bufs=12) as w_ops,
+        tc.tile_pool(name="x_ops", bufs=11) as x_ops,
+        tc.psum_pool(name="psum", bufs=PAIRS - 1) as psum,
     ):
         ident = consts.tile([P, P], F32)
         make_identity(nc, ident[:])
@@ -56,12 +56,14 @@ def tile_groupwiselinearprojector_k_kernel(tc, x, Wg, bg, out):
         bias_rows = consts.tile([P, P], F32)
         bias_sb = consts.tile([P, PAIRS], F32)
 
+        partial = [consts.tile([P, 4, P], F32, name=f"partial_{l}") for l in range(2)]
         result = [consts.tile([P, 4, 8, 2, 8], F32, name=f"result_{l}") for l in range(2)]
         out_sb = consts.tile([P, 8, 2, COLS], F32)
 
         raw_x, grouped_x, x_operand = {}, {}, {}
-        raw_w, w_operand = {}, {}
+        w_operand = {}
         grouped_w = {}
+        first_sums = {}
         sums = {}
 
         units = [("x", c) for c in range(LEAD)]
@@ -102,78 +104,82 @@ def tile_groupwiselinearprojector_k_kernel(tc, x, Wg, bg, out):
                     in_=values[:, part * width * PACK : (part + 1) * width * PACK],
                 )
 
-        def load_w(q):
-            a, first = q // 4, PIECE * (q % 4)
-            source = w_rows[a // 2, a % 2]
-            if q >= PIECES - ALONE:
-                channels = PIECE * K_PASS
-                tile = raw.tile([P, 2, channels], BF16, align_bytes=LOAD_ALIGN, name="raw_w", tag="raw")
-                nc.sync.dma_start(out=tile[:], in_=source[:, :, first * K_PASS : first * K_PASS + channels])
-                halves = [tile[:, z] for z in range(2)]
-            elif q % 2 == 0:
-                channels = 2 * PIECE * K_PASS
-                halves = []
-                for z in range(2):
-                    tile = raw.tile([P, channels], BF16, align_bytes=LOAD_ALIGN, name="raw_w", tag="raw")
-                    nc.sync.dma_start(out=tile[:], in_=source[:, z, first * K_PASS : first * K_PASS + channels])
-                    halves.append(tile[:])
-            else:
-                return
-            for c in range(channels // K_PASS):
-                raw_w[(a, first + c)] = [half[:, c * K_PASS : (c + 1) * K_PASS] for half in halves]
-
-        def transpose_w(q):
-            a, first = q // 4, PIECE * (q % 4)
-            grouped_w[q] = grouped.tile([P, PIECE * 2 * P * PACK], BF16, align_bytes=64, name="grouped_w", tag="grouped")
-            grouped_words = grouped_w[q][:].bitcast(F32).rearrange(
-                "p (c g z o u) -> p c g z o u", c=PIECE, g=2, z=2, o=OUT_CH
+        def prepare_w(q):
+            a, z = q // 2 % QUADS, q % 2
+            first = q // (2 * QUADS) * HALF
+            tile = raw.tile([P, HALF * K_PASS], BF16, align_bytes=LOAD_ALIGN, name="raw_w", tag="raw")
+            nc.sync.dma_start(
+                out=tile[:], in_=w_rows[a // 2, a % 2][:, z, first * K_PASS : (first + HALF) * K_PASS]
             )
-            for c in range(PIECE):
-                bank = psum.tile([P, 2, 2, P], F32, name="transposed", tag="bank")
-                for z in range(2):
-                    words = raw_w[(a, first + c)][z].bitcast(F32).rearrange("p (q u) -> p q u", u=2)
-                    for u in range(2):
-                        nc.tensor.transpose(bank[:, z, u, :], words[:, :, u], ident[:])
-                nc.scalar.copy(
-                    out=grouped_words[:, c],
-                    in_=bank[:].rearrange("p z u (g o) -> p g z o u", g=2),
+            words = tile[:].bitcast(F32).rearrange("p (c q u) -> p c q u", c=HALF, u=2)
+            for part in range(2):
+                if z == 0:
+                    grouped_w[(a, first + part * PART)] = grouped.tile(
+                        [P, PART * 2 * P * PACK], BF16, align_bytes=64, name="grouped_w", tag="grouped"
+                    )
+                grouped_words = grouped_w[(a, first + part * PART)][:].bitcast(F32).rearrange(
+                    "p (c g z o u) -> p c g z o u", c=PART, g=2, z=2, o=OUT_CH
                 )
+                for c in range(0, PART, 2):
+                    bank = psum.tile([P, 2, 2, P], F32, name="transposed", tag="bank")
+                    for n in range(2):
+                        for u in range(2):
+                            nc.tensor.transpose(bank[:, n, u, :], words[:, part * PART + c + n, :, u], ident[:])
+                    nc.scalar.copy(
+                        out=grouped_words[:, c : c + 2, :, z],
+                        in_=bank[:].rearrange("p n u (g o) -> p n g o u", g=2),
+                    )
 
-        def quantise_w(q):
-            a, first = q // 4, PIECE * (q % 4)
-            w_codes = w_ops.tile([P, PIECE * 2 * P], U32, align_bytes=64)
-            w_scales = w_ops.tile([P, PIECE * 2 * P], U8, align_bytes=64)
-            nc.vector.quantize_mx(out=w_codes[:].bitcast(FP8X4), scales=w_scales[:], in_=grouped_w[q][:])
-            for c in range(PIECE):
+        def quantise_w(a, first):
+            w_codes = w_ops.tile([P, PART * 2 * P], U32, align_bytes=64)
+            w_scales = w_ops.tile([P, PART * 2 * P], U8, align_bytes=64)
+            nc.vector.quantize_mx(out=w_codes[:].bitcast(FP8X4), scales=w_scales[:], in_=grouped_w[(a, first)][:])
+            for c in range(PART):
                 cols = slice(c * 2 * P, (c + 1) * 2 * P)
                 w_operand[(a, first + c)] = (w_codes[:, cols], w_scales[:, cols])
 
-        def multiply(c, pair):
-            if c == 0:
-                sums[pair] = psum.tile([P, P], F32, name="sums", tag="bank")
+        def multiply(c, pair, into):
             a, g2 = pair // 2, pair % 2
             w_codes, w_scales = w_operand[(a, c)]
             x_codes, x_scales = x_operand[c]
             m_cols = slice(g2 * P, (g2 + 1) * P)
             n_cols = slice(pair * P, (pair + 1) * P)
             nc.tensor.matmul_mx(
-                out=sums[pair][:],
+                out=into,
                 lhsT=w_codes[:, m_cols].bitcast(FP8X4),
                 lhsT_scale=w_scales[:, m_cols],
                 rhs=x_codes[:, n_cols].bitcast(FP8X4),
                 rhs_scale=x_scales[:, n_cols],
-                start=(c == 0),
-                stop=(c == LAST),
+                start=(c % HALF == 0),
+                stop=(c % HALF == HALF - 1),
             )
 
-        def add_bias(pair):
+        def multiply_first(a):
+            l = a // 2
+            if a % 2 == 0:
+                first_sums[l] = psum.tile([P, 4, P], F32, name="first_sums", tag="first", bufs=1)
+            for pair in (2 * a, 2 * a + 1):
+                for c in range(HALF):
+                    multiply(c, pair, first_sums[l][:, pair % 4, :])
+
+        def multiply_second(c, pair):
+            if c == HALF:
+                if pair < PAIRS - 1:
+                    sums[pair] = psum.tile([P, P], F32, name="sums", tag="bank")
+                else:
+                    sums[pair] = psum.tile([P, P], F32, name="last_sums", tag="first", bufs=1)
+            multiply(c, pair, sums[pair][:])
+
+        def finish(pair):
             l, i = pair // 4, pair % 4
-            to = result[l][:, i].rearrange("p n z w -> p (n z w)")
-            bias = bias_sb[:, pair : pair + 1]
-            if l == 0:
-                nc.scalar.activation(out=to, in_=sums[pair][:], func=IDENTITY, bias=bias)
-            else:
-                nc.vector.tensor_scalar_add(out=to, in0=sums[pair][:], scalar1=bias)
+            nc.vector.scalar_tensor_tensor(
+                out=result[l][:, i].rearrange("p n z w -> p (n z w)"),
+                in0=sums[pair][:],
+                scalar=bias_sb[:, pair : pair + 1],
+                in1=partial[l][:, i],
+                op0=ADD,
+                op1=ADD,
+            )
 
         def gather(l):
             copy = nc.scalar.copy if l == 0 else nc.vector.tensor_copy
@@ -195,18 +201,22 @@ def tile_groupwiselinearprojector_k_kernel(tc, x, Wg, bg, out):
                     )
 
         with tc.manual_schedule():
-            multiplied = 0
+            multiplied = HALF
             for s in range(len(units) + 1):
                 if s < len(units):
                     kind, index = units[s]
                     if kind == "w":
-                        load_w(index)
-                        transpose_w(index)
+                        a = index - 2 * QUADS - 1
+                        if a in (2, 4):
+                            nc.scalar.copy(out=partial[a // 2 - 1][:], in_=first_sums[a // 2 - 1][:])
+                        prepare_w(index)
+                        if 0 <= a < QUADS:
+                            multiply_first(a)
                     else:
                         load_x(index)
                         if index == LAST:
                             on_scalar = [(0, 1), (1, 1)]
-                        elif LEAD <= index < EARLY:
+                        elif LEAD <= index < EARLY - 1:
                             on_scalar = [(1, 1)]
                         else:
                             on_scalar = [(1, 0), (1, 1)]
@@ -219,20 +229,23 @@ def tile_groupwiselinearprojector_k_kernel(tc, x, Wg, bg, out):
                     nc.tensor.transpose(bias_ps[:], bias_rows[:], ident[:])
                 elif s == 5:
                     nc.vector.tensor_copy(out=bias_sb[:], in_=bias_ps[:, 0:PAIRS])
-                if s >= 2 and units[s - 2][0] == "w":
-                    quantise_w(units[s - 2][1])
+                for part in range(2):
+                    if s >= part + 1:
+                        kind, q = units[s - part - 1]
+                        if kind == "w" and q % 2 == 1:
+                            quantise_w(q // 2 % QUADS, q // (2 * QUADS) * HALF + part * PART)
                 if s >= 1 and units[s - 1][0] == "x":
                     c = units[s - 1][1]
                     quantise_x(c, parts=2 if c == LAST else 1)
                 if len(w_operand) == QUADS * PASSES:
                     for c in range(multiplied, min(len(x_operand), LAST)):
                         for pair in range(PAIRS):
-                            multiply(c, pair)
+                            multiply_second(c, pair)
                         multiplied = c + 1
             for l in range(2):
                 for i in range(4):
-                    multiply(LAST, 4 * l + i)
+                    multiply_second(LAST, 4 * l + i)
                 for i in range(4):
-                    add_bias(4 * l + i)
+                    finish(4 * l + i)
                 gather(l)
             store()

@@ -23,11 +23,7 @@ HALF = PASSES // 2
 PAIRS = 8
 QUADS = 4
 
-PIECES = 2 * QUADS * 2
-PART = HALF // 2
-
-LEAD = 2
-EARLY = 14
+PART = 4
 
 LOAD_ALIGN = 256
 
@@ -42,7 +38,7 @@ def tile_groupwiselinearprojector_k_kernel(tc, x, Wg, bg, out):
         tc.tile_pool(name="grouped", bufs=6) as grouped,
         tc.tile_pool(name="w_ops", bufs=12) as w_ops,
         tc.tile_pool(name="x_ops", bufs=11) as x_ops,
-        tc.psum_pool(name="psum", bufs=PAIRS - 1) as psum,
+        tc.psum_pool(name="psum", bufs=6) as psum,
     ):
         ident = consts.tile([P, P], F32)
         make_identity(nc, ident[:])
@@ -56,22 +52,23 @@ def tile_groupwiselinearprojector_k_kernel(tc, x, Wg, bg, out):
         bias_rows = consts.tile([P, P], F32)
         bias_sb = consts.tile([P, PAIRS], F32)
 
-        partial = [consts.tile([P, 4, P], F32, name=f"partial_{l}") for l in range(2)]
-        result = [consts.tile([P, 4, 8, 2, 8], F32, name=f"result_{l}") for l in range(2)]
         out_sb = consts.tile([P, 8, 2, COLS], F32)
 
         raw_x, grouped_x, x_operand = {}, {}, {}
         w_operand = {}
         grouped_w = {}
-        first_sums = {}
         sums = {}
+        added = [0, 0]
 
-        units = [("x", c) for c in range(LEAD)]
-        spread = EARLY - LEAD
-        for q in range(PIECES):
-            units.append(("w", q))
-            units += [("x", LEAD + n) for n in range(q * spread // PIECES, (q + 1) * spread // PIECES)]
-        units += [("x", c) for c in range(EARLY, PASSES)]
+        units = [("x", c) for c in range(2)]
+        taken = 2
+        pieces = [(a, z, n) for n in range(2) for a in range(QUADS) for z in range(2)]
+        for q, piece in enumerate(pieces):
+            units.append(("w", *piece))
+            if q < 12 or q % 2 == 1:
+                units.append(("x", taken))
+                taken += 1
+        units += [("x", c) for c in range(taken, PASSES)]
 
         def load_x(c):
             raw_x[c] = raw.tile([P, BATCH, PACK, PIXELS], BF16, align_bytes=LOAD_ALIGN, name="raw_x", tag="raw")
@@ -104,20 +101,19 @@ def tile_groupwiselinearprojector_k_kernel(tc, x, Wg, bg, out):
                     in_=values[:, part * width * PACK : (part + 1) * width * PACK],
                 )
 
-        def prepare_w(q):
-            a, z = q // 2 % QUADS, q % 2
-            first = q // (2 * QUADS) * HALF
+        def prepare_w(a, z, half):
             tile = raw.tile([P, HALF * K_PASS], BF16, align_bytes=LOAD_ALIGN, name="raw_w", tag="raw")
             nc.sync.dma_start(
-                out=tile[:], in_=w_rows[a // 2, a % 2][:, z, first * K_PASS : (first + HALF) * K_PASS]
+                out=tile[:], in_=w_rows[a // 2, a % 2][:, z, half * HALF * K_PASS : (half + 1) * HALF * K_PASS]
             )
             words = tile[:].bitcast(F32).rearrange("p (c q u) -> p c q u", c=HALF, u=2)
             for part in range(2):
+                key = (a, half * HALF + part * PART)
                 if z == 0:
-                    grouped_w[(a, first + part * PART)] = grouped.tile(
+                    grouped_w[key] = grouped.tile(
                         [P, PART * 2 * P * PACK], BF16, align_bytes=64, name="grouped_w", tag="grouped"
                     )
-                grouped_words = grouped_w[(a, first + part * PART)][:].bitcast(F32).rearrange(
+                grouped_words = grouped_w[key][:].bitcast(F32).rearrange(
                     "p (c g z o u) -> p c g z o u", c=PART, g=2, z=2, o=OUT_CH
                 )
                 for c in range(0, PART, 2):
@@ -137,57 +133,54 @@ def tile_groupwiselinearprojector_k_kernel(tc, x, Wg, bg, out):
             for c in range(PART):
                 cols = slice(c * 2 * P, (c + 1) * 2 * P)
                 w_operand[(a, first + c)] = (w_codes[:, cols], w_scales[:, cols])
+            return [(first + c, pair) for c in range(PART) for pair in (2 * a, 2 * a + 1) if first + c in x_operand]
 
-        def multiply(c, pair, into):
+        def open_sums():
+            zeros = consts.tile([P, P * PACK], BF16, align_bytes=64)
+            zero_codes = consts.tile([P, P], U32, align_bytes=64)
+            zero_scales = consts.tile([P, P], U8, align_bytes=64)
+            nc.vector.memset(zeros[:], 0.0)
+            nc.vector.quantize_mx(out=zero_codes[:].bitcast(FP8X4), scales=zero_scales[:], in_=zeros[:])
+            x_codes, x_scales = x_operand[0]
+            for l in range(2):
+                sums[l] = psum.tile([P, 4, P], F32, name=f"sums_{l}", tag=f"sums_{l}", bufs=1)
+                cols = slice(l * 4 * P, (l + 1) * 4 * P)
+                nc.tensor.matmul_mx(
+                    out=sums[l][:].rearrange("p i n -> p (i n)"),
+                    lhsT=zero_codes[:].bitcast(FP8X4),
+                    lhsT_scale=zero_scales[:],
+                    rhs=x_codes[:, cols].bitcast(FP8X4),
+                    rhs_scale=x_scales[:, cols],
+                    start=True,
+                    stop=False,
+                )
+
+        def multiply(c, pair):
             a, g2 = pair // 2, pair % 2
+            l, i = pair // 4, pair % 4
             w_codes, w_scales = w_operand[(a, c)]
             x_codes, x_scales = x_operand[c]
             m_cols = slice(g2 * P, (g2 + 1) * P)
             n_cols = slice(pair * P, (pair + 1) * P)
+            added[l] += 1
             nc.tensor.matmul_mx(
-                out=into,
+                out=sums[l][:, i],
                 lhsT=w_codes[:, m_cols].bitcast(FP8X4),
                 lhsT_scale=w_scales[:, m_cols],
                 rhs=x_codes[:, n_cols].bitcast(FP8X4),
                 rhs_scale=x_scales[:, n_cols],
-                start=(c % HALF == 0),
-                stop=(c % HALF == HALF - 1),
+                start=False,
+                stop=(added[l] == 4 * PASSES),
             )
 
-        def multiply_first(a):
-            l = a // 2
-            if a % 2 == 0:
-                first_sums[l] = psum.tile([P, 4, P], F32, name="first_sums", tag="first", bufs=1)
-            for pair in (2 * a, 2 * a + 1):
-                for c in range(HALF):
-                    multiply(c, pair, first_sums[l][:, pair % 4, :])
-
-        def multiply_second(c, pair):
-            if c == HALF:
-                if pair < PAIRS - 1:
-                    sums[pair] = psum.tile([P, P], F32, name="sums", tag="bank")
-                else:
-                    sums[pair] = psum.tile([P, P], F32, name="last_sums", tag="first", bufs=1)
-            multiply(c, pair, sums[pair][:])
-
-        def finish(pair):
-            l, i = pair // 4, pair % 4
-            nc.vector.scalar_tensor_tensor(
-                out=result[l][:, i].rearrange("p n z w -> p (n z w)"),
-                in0=sums[pair][:],
-                scalar=bias_sb[:, pair : pair + 1],
-                in1=partial[l][:, i],
-                op0=ADD,
-                op1=ADD,
-            )
-
-        def gather(l):
-            copy = nc.scalar.copy if l == 0 else nc.vector.tensor_copy
+        def finish(l):
             for z in range(2):
                 rows = slice(z * OUT_CH, (z + 1) * OUT_CH)
-                copy(
+                bias = bias_sb[rows, 4 * l : 4 * l + 4].unsqueeze(1).unsqueeze(1)
+                nc.vector.tensor_add(
                     out=out_sb[rows, :, l, :].rearrange("p n (w i) -> p n w i", i=4),
-                    in_=result[l][rows, :, :, z, :].rearrange("p i n w -> p n w i"),
+                    in0=sums[l][rows].rearrange("p i (n y w) -> p y n w i", y=2, w=8)[:, z],
+                    in1=bias.to_broadcast([OUT_CH, 8, 8, 4]),
                 )
 
         def store():
@@ -201,51 +194,48 @@ def tile_groupwiselinearprojector_k_kernel(tc, x, Wg, bg, out):
                     )
 
         with tc.manual_schedule():
-            multiplied = HALF
-            for s in range(len(units) + 1):
+            ready = []
+            for s in range(len(units) + 2):
                 if s < len(units):
-                    kind, index = units[s]
+                    kind, *rest = units[s]
                     if kind == "w":
-                        a = index - 2 * QUADS - 1
-                        if a in (2, 4):
-                            nc.scalar.copy(out=partial[a // 2 - 1][:], in_=first_sums[a // 2 - 1][:])
-                        prepare_w(index)
-                        if 0 <= a < QUADS:
-                            multiply_first(a)
+                        prepare_w(*rest)
                     else:
-                        load_x(index)
-                        if index == LAST:
+                        c = rest[0]
+                        load_x(c)
+                        if c == LAST:
                             on_scalar = [(0, 1), (1, 1)]
-                        elif LEAD <= index < EARLY - 1:
+                        elif c % 2 == 0:
                             on_scalar = [(1, 1)]
                         else:
                             on_scalar = [(1, 0), (1, 1)]
-                        regroup_x(index, on_scalar)
+                        regroup_x(c, on_scalar)
                 if s == 1:
                     nc.vector.memset(bias_rows[:], 0.0)
                     nc.vector.tensor_copy(out=bias_rows[0:PAIRS, :], in_=bg_sb[:])
                 elif s == 3:
                     bias_ps = psum.tile([P, P], F32, name="bias_ps", tag="bank")
                     nc.tensor.transpose(bias_ps[:], bias_rows[:], ident[:])
+                    open_sums()
                 elif s == 5:
                     nc.vector.tensor_copy(out=bias_sb[:], in_=bias_ps[:, 0:PAIRS])
-                for part in range(2):
-                    if s >= part + 1:
-                        kind, q = units[s - part - 1]
-                        if kind == "w" and q % 2 == 1:
-                            quantise_w(q // 2 % QUADS, q // (2 * QUADS) * HALF + part * PART)
-                if s >= 1 and units[s - 1][0] == "x":
-                    c = units[s - 1][1]
-                    quantise_x(c, parts=2 if c == LAST else 1)
-                if len(w_operand) == QUADS * PASSES:
-                    for c in range(multiplied, min(len(x_operand), LAST)):
-                        for pair in range(PAIRS):
-                            multiply_second(c, pair)
-                        multiplied = c + 1
+                if s >= 2:
+                    for c, pair in ready[s - 2]:
+                        multiply(c, pair)
+                new = []
+                for back in (2, 1):
+                    if back <= s < len(units) + back:
+                        kind, *rest = units[s - back]
+                        if kind == "w" and rest[1] == 1:
+                            new += quantise_w(rest[0], rest[2] * HALF + (back - 1) * PART)
+                        elif kind == "x" and back == 1:
+                            c = rest[0]
+                            quantise_x(c, parts=2 if s >= len(units) else 1)
+                            new += [(c, pair) for pair in range(PAIRS) if (pair // 2, c) in w_operand]
+                ready.append(new)
+            for new in ready[-2:]:
+                for c, pair in new:
+                    multiply(c, pair)
             for l in range(2):
-                for i in range(4):
-                    multiply_second(LAST, 4 * l + i)
-                for i in range(4):
-                    finish(4 * l + i)
-                gather(l)
+                finish(l)
             store()

@@ -34,10 +34,10 @@ def tile_groupwiselinearprojector_k_kernel(tc, x, Wg, bg, out):
 
     with (
         tc.tile_pool(name="consts", bufs=1) as consts,
-        tc.tile_pool(name="raw", bufs=7) as raw,
-        tc.tile_pool(name="grouped", bufs=6) as grouped,
-        tc.tile_pool(name="w_ops", bufs=12) as w_ops,
-        tc.tile_pool(name="x_ops", bufs=11) as x_ops,
+        tc.tile_pool(name="raw", bufs=6) as raw,
+        tc.tile_pool(name="grouped", bufs=5) as grouped,
+        tc.tile_pool(name="w_ops", bufs=14) as w_ops,
+        tc.tile_pool(name="x_ops", bufs=12) as x_ops,
         tc.psum_pool(name="psum", bufs=6) as psum,
     ):
         ident = consts.tile([P, P], F32)
@@ -60,15 +60,14 @@ def tile_groupwiselinearprojector_k_kernel(tc, x, Wg, bg, out):
         sums = {}
         added = [0, 0]
 
+        pieces = [("z", a, z, n) for n in range(2) for a in range(QUADS) for z in range(2)][:-2]
         units = [("x", c) for c in range(2)]
-        taken = 2
-        pieces = [(a, z, n) for n in range(2) for a in range(QUADS) for z in range(2)]
         for q, piece in enumerate(pieces):
-            units.append(("w", *piece))
-            if q < 12 or q % 2 == 1:
-                units.append(("x", taken))
-                taken += 1
-        units += [("x", c) for c in range(taken, PASSES)]
+            units.append(piece)
+            if q + 2 < LAST - 1:
+                units.append(("x", q + 2))
+        units += [("x", LAST - 1), ("c", QUADS - 1, HALF, 4), ("x", LAST)]
+        units += [("c", QUADS - 1, HALF + 4, 2), ("c", QUADS - 1, HALF + 6, 2)]
 
         def load_x(c):
             raw_x[c] = raw.tile([P, BATCH, PACK, PIXELS], BF16, align_bytes=LOAD_ALIGN, name="raw_x", tag="raw")
@@ -101,7 +100,14 @@ def tile_groupwiselinearprojector_k_kernel(tc, x, Wg, bg, out):
                     in_=values[:, part * width * PACK : (part + 1) * width * PACK],
                 )
 
-        def prepare_w(a, z, half):
+        def transpose_bank(bank, slot, words):
+            for u in range(2):
+                nc.tensor.transpose(bank[:, slot, u, :], words[:, :, u], ident[:])
+
+        def grouped_words(tile, count):
+            return tile[:].bitcast(F32).rearrange("p (c g z o u) -> p c g z o u", c=count, g=2, z=2, o=OUT_CH)
+
+        def prepare_w_rows(a, z, half):
             tile = raw.tile([P, HALF * K_PASS], BF16, align_bytes=LOAD_ALIGN, name="raw_w", tag="raw")
             nc.sync.dma_start(
                 out=tile[:], in_=w_rows[a // 2, a % 2][:, z, half * HALF * K_PASS : (half + 1) * HALF * K_PASS]
@@ -113,27 +119,45 @@ def tile_groupwiselinearprojector_k_kernel(tc, x, Wg, bg, out):
                     grouped_w[key] = grouped.tile(
                         [P, PART * 2 * P * PACK], BF16, align_bytes=64, name="grouped_w", tag="grouped"
                     )
-                grouped_words = grouped_w[key][:].bitcast(F32).rearrange(
-                    "p (c g z o u) -> p c g z o u", c=PART, g=2, z=2, o=OUT_CH
-                )
                 for c in range(0, PART, 2):
                     bank = psum.tile([P, 2, 2, P], F32, name="transposed", tag="bank")
                     for n in range(2):
-                        for u in range(2):
-                            nc.tensor.transpose(bank[:, n, u, :], words[:, part * PART + c + n, :, u], ident[:])
+                        transpose_bank(bank, n, words[:, part * PART + c + n])
                     nc.scalar.copy(
-                        out=grouped_words[:, c : c + 2, :, z],
+                        out=grouped_words(grouped_w[key], PART)[:, c : c + 2, :, z],
                         in_=bank[:].rearrange("p n u (g o) -> p n g o u", g=2),
                     )
 
-        def quantise_w(a, first):
+        def prepare_w_passes(a, first, count):
+            tile = raw.tile([P, 2, count * K_PASS], BF16, align_bytes=LOAD_ALIGN, name="raw_w", tag="raw")
+            nc.sync.dma_start(
+                out=tile[:], in_=w_rows[a // 2, a % 2][:, :, first * K_PASS : (first + count) * K_PASS]
+            )
+            words = tile[:].bitcast(F32).rearrange("p z (c q u) -> p z c q u", c=count, u=2)
+            grouped_w[(a, first)] = grouped.tile(
+                [P, count * 2 * P * PACK], BF16, align_bytes=64, name="grouped_w", tag="grouped"
+            )
+            for c in range(count):
+                bank = psum.tile([P, 2, 2, P], F32, name="transposed", tag="bank")
+                for z in range(2):
+                    transpose_bank(bank, z, words[:, z, c])
+                copy = nc.scalar.copy
+                copy(
+                    out=grouped_words(grouped_w[(a, first)], count)[:, c],
+                    in_=bank[:].rearrange("p z u (g o) -> p g z o u", g=2),
+                )
+
+        def quantise_w(a, first, count):
             w_codes = w_ops.tile([P, PART * 2 * P], U32, align_bytes=64)
             w_scales = w_ops.tile([P, PART * 2 * P], U8, align_bytes=64)
-            nc.vector.quantize_mx(out=w_codes[:].bitcast(FP8X4), scales=w_scales[:], in_=grouped_w[(a, first)][:])
-            for c in range(PART):
+            width = count * 2 * P
+            nc.vector.quantize_mx(
+                out=w_codes[:, :width].bitcast(FP8X4), scales=w_scales[:, :width], in_=grouped_w[(a, first)][:]
+            )
+            for c in range(count):
                 cols = slice(c * 2 * P, (c + 1) * 2 * P)
                 w_operand[(a, first + c)] = (w_codes[:, cols], w_scales[:, cols])
-            return [(first + c, pair) for c in range(PART) for pair in (2 * a, 2 * a + 1) if first + c in x_operand]
+            return [(first + c, pair) for c in range(count) for pair in (2 * a, 2 * a + 1) if first + c in x_operand]
 
         def open_sums():
             zeros = consts.tile([P, P * PACK], BF16, align_bytes=64)
@@ -195,21 +219,17 @@ def tile_groupwiselinearprojector_k_kernel(tc, x, Wg, bg, out):
 
         with tc.manual_schedule():
             ready = []
-            for s in range(len(units) + 2):
+            for s in range(len(units) + 1):
                 if s < len(units):
                     kind, *rest = units[s]
-                    if kind == "w":
-                        prepare_w(*rest)
+                    if kind == "z":
+                        prepare_w_rows(*rest)
+                    elif kind == "c":
+                        prepare_w_passes(*rest)
                     else:
                         c = rest[0]
                         load_x(c)
-                        if c == LAST:
-                            on_scalar = [(0, 1), (1, 1)]
-                        elif c % 2 == 0:
-                            on_scalar = [(1, 1)]
-                        else:
-                            on_scalar = [(1, 0), (1, 1)]
-                        regroup_x(c, on_scalar)
+                        regroup_x(c, [(1, 1)] if c % 2 == 0 or c == LAST else [(1, 0), (1, 1)])
                 if s == 1:
                     nc.vector.memset(bias_rows[:], 0.0)
                     nc.vector.tensor_copy(out=bias_rows[0:PAIRS, :], in_=bg_sb[:])
@@ -219,23 +239,23 @@ def tile_groupwiselinearprojector_k_kernel(tc, x, Wg, bg, out):
                     open_sums()
                 elif s == 5:
                     nc.vector.tensor_copy(out=bias_sb[:], in_=bias_ps[:, 0:PAIRS])
-                if s >= 2:
-                    for c, pair in ready[s - 2]:
+                if s < len(units) - 2 or s == len(units):
+                    for c, pair in ready:
                         multiply(c, pair)
-                new = []
+                    ready = []
                 for back in (2, 1):
-                    if back <= s < len(units) + back:
+                    if back <= s:
                         kind, *rest = units[s - back]
-                        if kind == "w" and rest[1] == 1:
-                            new += quantise_w(rest[0], rest[2] * HALF + (back - 1) * PART)
+                        if kind == "z" and rest[1] == 1:
+                            ready += quantise_w(rest[0], rest[2] * HALF + (back - 1) * PART, PART)
+                        elif kind == "c" and back == 1:
+                            ready += quantise_w(*rest)
                         elif kind == "x" and back == 1:
                             c = rest[0]
-                            quantise_x(c, parts=2 if s >= len(units) else 1)
-                            new += [(c, pair) for pair in range(PAIRS) if (pair // 2, c) in w_operand]
-                ready.append(new)
-            for new in ready[-2:]:
-                for c, pair in new:
-                    multiply(c, pair)
+                            quantise_x(c, parts=1)
+                            ready += [(c, pair) for pair in range(PAIRS) if (pair // 2, c) in w_operand]
+            for c, pair in ready:
+                multiply(c, pair)
             for l in range(2):
                 finish(l)
             store()

@@ -25,6 +25,8 @@ QUADS = 4
 
 PART = 4
 
+LATE = 13
+
 LOAD_ALIGN = 256
 
 
@@ -78,7 +80,7 @@ def tile_groupwiselinearprojector_k_kernel(tc, x, Wg, bg, out):
                 )
 
         def regroup_x(c, on_scalar):
-            grouped_x[c] = grouped.tile([P, 2, 4, P, PACK], BF16, align_bytes=64, name="grouped_x", tag="grouped")
+            grouped_x[c] = grouped.tile([P, 2, 4, P, PACK], BF16, align_bytes=64, name="grouped_x", tag="grouped_x", bufs=2)
             src = raw_x[c][:].rearrange("p b t (a l w i) -> p b l a w t i", a=8, l=2, i=4)
             dst = grouped_x[c][:].rearrange("p l i (b a w) t -> p b l a w t i", b=BATCH, a=8)
             for b in range(BATCH):
@@ -117,7 +119,7 @@ def tile_groupwiselinearprojector_k_kernel(tc, x, Wg, bg, out):
                 key = (a, half * HALF + part * PART)
                 if z == 0:
                     grouped_w[key] = grouped.tile(
-                        [P, PART * 2 * P * PACK], BF16, align_bytes=64, name="grouped_w", tag="grouped"
+                        [P, PART * 2 * P * PACK], BF16, align_bytes=64, name="grouped_w", tag="grouped_w", bufs=3
                     )
                 for c in range(0, PART, 2):
                     bank = psum.tile([P, 2, 2, P], F32, name="transposed", tag="bank")
@@ -135,7 +137,7 @@ def tile_groupwiselinearprojector_k_kernel(tc, x, Wg, bg, out):
             )
             words = tile[:].bitcast(F32).rearrange("p z (c q u) -> p z c q u", c=count, u=2)
             grouped_w[(a, first)] = grouped.tile(
-                [P, count * 2 * P * PACK], BF16, align_bytes=64, name="grouped_w", tag="grouped"
+                [P, count * 2 * P * PACK], BF16, align_bytes=64, name="grouped_w", tag="grouped_w", bufs=3
             )
             for c in range(count):
                 bank = psum.tile([P, 2, 2, P], F32, name="transposed", tag="bank")
@@ -229,7 +231,7 @@ def tile_groupwiselinearprojector_k_kernel(tc, x, Wg, bg, out):
                     else:
                         c = rest[0]
                         load_x(c)
-                        regroup_x(c, [(1, 1)] if c % 2 == 0 or c == LAST else [(1, 0), (1, 1)])
+                        regroup_x(c, [(1, 1)] if c % 2 == 0 or c >= LATE else [(1, 0), (1, 1)])
                 if s == 1:
                     nc.vector.memset(bias_rows[:], 0.0)
                     nc.vector.tensor_copy(out=bias_rows[0:PAIRS, :], in_=bg_sb[:])

import concourse.mybir as mybir
from concourse.masks import make_identity

FLOPS = 2 * 16 * 64 * 64 * 8192

F32 = mybir.dt.float32
BF16 = mybir.dt.bfloat16
U32 = mybir.dt.uint32
U8 = mybir.dt.uint8
FP8X4 = mybir.dt.float8_e4m3fn_x4
ADD = mybir.AluOpType.add

P = 128
PACK = 4
K_PASS = P * PACK

BATCH, CHANNELS, OUT_CH, ROWS, COLS = 2, 8192, 64, 16, 32
PIXELS = ROWS * COLS
PASSES = CHANNELS // K_PASS
LAST = PASSES - 1
HALF = PASSES // 2

PAIRS = 8
QUADS = 4

PART = 4

LATE = 13

LOAD_ALIGN = 256


def tile_groupwiselinearprojector_k_kernel(tc, x, Wg, bg, out):
    nc = tc.nc
    w_rows = Wg.rearrange("g o k -> (g o) k").rearrange("(z l e p) k -> l e p z k", l=2, z=2, e=2)

    with (
        tc.tile_pool(name="consts", bufs=1) as consts,
        tc.tile_pool(name="raw", bufs=6) as raw,
        tc.tile_pool(name="grouped", bufs=5) as grouped,
        tc.tile_pool(name="w_ops", bufs=14) as w_ops,
        tc.tile_pool(name="x_ops", bufs=12) as x_ops,
        tc.psum_pool(name="psum", bufs=6) as psum,
    ):
        ident = consts.tile([P, P], F32)
        make_identity(nc, ident[:])

        bg_sb = consts.tile([PAIRS, P], BF16)
        for l in range(2):
            nc.scalar.dma_start(
                out=bg_sb[4 * l : 4 * l + 4, :].rearrange("i (z o) -> i z o", z=2),
                in_=bg.rearrange("(z l i) o -> l i z o", l=2, z=2)[l],
            )
        bias_rows = consts.tile([P, P], F32)
        bias_sb = consts.tile([P, PAIRS], F32)

        out_sb = consts.tile([P, 8, 2, COLS], F32)

        raw_x, grouped_x, x_operand = {}, {}, {}
        w_operand = {}
        grouped_w = {}
        sums = {}
        added = [0, 0]

        pieces = [("z", a, z, n) for n in range(2) for a in range(QUADS) for z in range(2)][:-2]
        units = [("x", c) for c in range(2)]
        for q, piece in enumerate(pieces):
            units.append(piece)
            if q + 2 < LAST - 1:
                units.append(("x", q + 2))
        units += [("x", LAST - 1), ("c", QUADS - 1, HALF, 4), ("x", LAST)]
        units += [("c", QUADS - 1, HALF + 4, 2), ("c", QUADS - 1, HALF + 6, 2)]

        def load_x(c):
            raw_x[c] = raw.tile([P, BATCH, PACK, PIXELS], BF16, align_bytes=LOAD_ALIGN, name="raw_x", tag="raw")
            for b in range(BATCH):
                nc.sync.dma_start(
                    out=raw_x[c][:, b].rearrange("p t x -> p (t x)"),
                    in_=x[b, c * K_PASS : (c + 1) * K_PASS].rearrange("(p t) r w -> p (t r w)", t=PACK),
                )

        def regroup_x(c, on_scalar):
            grouped_x[c] = grouped.tile([P, 2, 4, P, PACK], BF16, align_bytes=64, name="grouped_x", tag="grouped_x", bufs=2)
            src = raw_x[c][:].rearrange("p b t (a l w i) -> p b l a w t i", a=8, l=2, i=4)
            dst = grouped_x[c][:].rearrange("p l i (b a w) t -> p b l a w t i", b=BATCH, a=8)
            for b in range(BATCH):
                for l in range(2):
                    copy = nc.scalar.copy if (b, l) in on_scalar else nc.vector.tensor_copy
                    copy(out=dst[:, b, l], in_=src[:, b, l])

        def quantise_x(c, parts):
            x_codes = x_ops.tile([P, PAIRS * P], U32, align_bytes=64)
            x_scales = x_ops.tile([P, PAIRS * P], U8, align_bytes=64)
            x_operand[c] = (x_codes, x_scales)
            values = grouped_x[c][:].rearrange("p l i m t -> p (l i m t)")
            width = PAIRS * P // parts
            for part in range(parts):
                cols = slice(part * width, (part + 1) * width)
                nc.vector.quantize_mx(
                    out=x_codes[:, cols].bitcast(FP8X4),
                    scales=x_scales[:, cols],
                    in_=values[:, part * width * PACK : (part + 1) * width * PACK],
                )

        def transpose_bank(bank, slot, words):
            for u in range(2):
                nc.tensor.transpose(bank[:, slot, u, :], words[:, :, u], ident[:])

        def grouped_words(tile, count):
            return tile[:].bitcast(F32).rearrange("p (c g z o u) -> p c g z o u", c=count, g=2, z=2, o=OUT_CH)

        def prepare_w_rows(a, z, half):
            tile = raw.tile([P, HALF * K_PASS], BF16, align_bytes=LOAD_ALIGN, name="raw_w", tag="raw")
            nc.sync.dma_start(
                out=tile[:], in_=w_rows[a // 2, a % 2][:, z, half * HALF * K_PASS : (half + 1) * HALF * K_PASS]
            )
            words = tile[:].bitcast(F32).rearrange("p (c q u) -> p c q u", c=HALF, u=2)
            for part in range(2):
                key = (a, half * HALF + part * PART)
                if z == 0:
                    grouped_w[key] = grouped.tile(
                        [P, PART * 2 * P * PACK], BF16, align_bytes=64, name="grouped_w", tag="grouped_w", bufs=3
                    )
                for c in range(0, PART, 2):
                    bank = psum.tile([P, 2, 2, P], F32, name="transposed", tag="bank")
                    for n in range(2):
                        transpose_bank(bank, n, words[:, part * PART + c + n])
                    nc.scalar.copy(
                        out=grouped_words(grouped_w[key], PART)[:, c : c + 2, :, z],
                        in_=bank[:].rearrange("p n u (g o) -> p n g o u", g=2),
                    )

        def prepare_w_passes(a, first, count):
            tile = raw.tile([P, 2, count * K_PASS], BF16, align_bytes=LOAD_ALIGN, name="raw_w", tag="raw")
            nc.sync.dma_start(
                out=tile[:], in_=w_rows[a // 2, a % 2][:, :, first * K_PASS : (first + count) * K_PASS]
            )
            words = tile[:].bitcast(F32).rearrange("p z (c q u) -> p z c q u", c=count, u=2)
            grouped_w[(a, first)] = grouped.tile(
                [P, count * 2 * P * PACK], BF16, align_bytes=64, name="grouped_w", tag="grouped_w", bufs=3
            )
            for c in range(count):
                bank = psum.tile([P, 2, 2, P], F32, name="transposed", tag="bank")
                for z in range(2):
                    transpose_bank(bank, z, words[:, z, c])
                copy = nc.scalar.copy
                copy(
                    out=grouped_words(grouped_w[(a, first)], count)[:, c],
                    in_=bank[:].rearrange("p z u (g o) -> p g z o u", g=2),
                )

        def quantise_w(a, first, count):
            w_codes = w_ops.tile([P, PART * 2 * P], U32, align_bytes=64)
            w_scales = w_ops.tile([P, PART * 2 * P], U8, align_bytes=64)
            width = count * 2 * P
            nc.vector.quantize_mx(
                out=w_codes[:, :width].bitcast(FP8X4), scales=w_scales[:, :width], in_=grouped_w[(a, first)][:]
            )
            for c in range(count):
                cols = slice(c * 2 * P, (c + 1) * 2 * P)
                w_operand[(a, first + c)] = (w_codes[:, cols], w_scales[:, cols])
            return [(first + c, pair) for c in range(count) for pair in (2 * a, 2 * a + 1) if first + c in x_operand]

        def open_sums():
            zeros = consts.tile([P, P * PACK], BF16, align_bytes=64)
            zero_codes = consts.tile([P, P], U32, align_bytes=64)
            zero_scales = consts.tile([P, P], U8, align_bytes=64)
            nc.vector.memset(zeros[:], 0.0)
            nc.vector.quantize_mx(out=zero_codes[:].bitcast(FP8X4), scales=zero_scales[:], in_=zeros[:])
            x_codes, x_scales = x_operand[0]
            for l in range(2):
                sums[l] = psum.tile([P, 4, P], F32, name=f"sums_{l}", tag=f"sums_{l}", bufs=1)
                cols = slice(l * 4 * P, (l + 1) * 4 * P)
                nc.tensor.matmul_mx(
                    out=sums[l][:].rearrange("p i n -> p (i n)"),
                    lhsT=zero_codes[:].bitcast(FP8X4),
                    lhsT_scale=zero_scales[:],
                    rhs=x_codes[:, cols].bitcast(FP8X4),
                    rhs_scale=x_scales[:, cols],
                    start=True,
                    stop=False,
                )

        def multiply(c, pair):
            a, g2 = pair // 2, pair % 2
            l, i = pair // 4, pair % 4
            w_codes, w_scales = w_operand[(a, c)]
            x_codes, x_scales = x_operand[c]
            m_cols = slice(g2 * P, (g2 + 1) * P)
            n_cols = slice(pair * P, (pair + 1) * P)
            added[l] += 1
            nc.tensor.matmul_mx(
                out=sums[l][:, i],
                lhsT=w_codes[:, m_cols].bitcast(FP8X4),
                lhsT_scale=w_scales[:, m_cols],
                rhs=x_codes[:, n_cols].bitcast(FP8X4),
                rhs_scale=x_scales[:, n_cols],
                start=False,
                stop=(added[l] == 4 * PASSES),
            )

        def finish(l):
            for z in range(2):
                rows = slice(z * OUT_CH, (z + 1) * OUT_CH)
                bias = bias_sb[rows, 4 * l : 4 * l + 4].unsqueeze(1).unsqueeze(1)
                nc.vector.tensor_add(
                    out=out_sb[rows, :, l, :].rearrange("p n (w i) -> p n w i", i=4),
                    in0=sums[l][rows].rearrange("p i (n y w) -> p y n w i", y=2, w=8)[:, z],
                    in1=bias.to_broadcast([OUT_CH, 8, 8, 4]),
                )

        def store():
            for z in range(2):
                rows = slice(z * OUT_CH, (z + 1) * OUT_CH)
                queue = nc.sync if z == 0 else nc.scalar
                for b in range(BATCH):
                    queue.dma_start(
                        out=out[b].rearrange("o (h z l) c -> z o h (l c)", l=2, z=2)[z],
                        in_=out_sb[rows, 4 * b : 4 * b + 4].rearrange("p n l c -> p n (l c)"),
                    )

        with tc.manual_schedule():
            ready = []
            for s in range(len(units) + 1):
                if s < len(units):
                    kind, *rest = units[s]
                    if kind == "z":
                        prepare_w_rows(*rest)
                    elif kind == "c":
                        prepare_w_passes(*rest)
                    else:
                        c = rest[0]
                        load_x(c)
                        regroup_x(c, [(1, 1)] if c % 2 == 0 or c >= LATE else [(1, 0), (1, 1)])
                if s == 1:
                    nc.vector.memset(bias_rows[:], 0.0)
                    nc.vector.tensor_copy(out=bias_rows[0:PAIRS, :], in_=bg_sb[:])
                elif s == 3:
                    bias_ps = psum.tile([P, P], F32, name="bias_ps", tag="bank")
                    nc.tensor.transpose(bias_ps[:], bias_rows[:], ident[:])
                    open_sums()
                elif s == 5:
                    nc.vector.tensor_copy(out=bias_sb[:], in_=bias_ps[:, 0:PAIRS])
                if s < len(units) - 2 or s == len(units):
                    for c, pair in ready:
                        multiply(c, pair)
                    ready = []
                for back in (2, 1):
                    if back <= s:
                        kind, *rest = units[s - back]
                        if kind == "z" and rest[1] == 1:
                            ready += quantise_w(rest[0], rest[2] * HALF + (back - 1) * PART, PART)
                        elif kind == "c" and back == 1:
                            ready += quantise_w(*rest)
                        elif kind == "x" and back == 1:
                            c = rest[0]
                            quantise_x(c, parts=1)
                            ready += [(c, pair) for pair in range(PAIRS) if (pair // 2, c) in w_operand]
            for c, pair in ready:
                multiply(c, pair)
            for l in range(2):
                finish(l)
            store()
